import numpy as np
import ml_dtypes


def mxq(x, axis, fmt="e4m3"):
    dtype, down = {"e4m3": (ml_dtypes.float8_e4m3fn, 7), "e5m2": (ml_dtypes.float8_e5m2, 14)}[fmt]
    v = np.moveaxis(np.asarray(x, np.float32).astype(ml_dtypes.bfloat16).astype(np.float64), axis, -1)
    blocks = v.reshape(v.shape[:-1] + (-1, 32))
    amax = np.abs(blocks).max(-1, keepdims=True)
    byte = np.maximum(np.where(amax > 0, np.frexp(amax)[1] - 1 + 127, 0) - down, 1)
    scale = np.exp2(byte - 127.0)
    codes = (blocks / scale).astype(np.float32).astype(dtype).astype(np.float64)
    return np.moveaxis((codes * scale).reshape(v.shape), -1, axis)


WIDE = False


def mx_kscale(k):
    if not WIDE:
        return np.ones(k)
    levels = np.array([10, -10, 5, -5, 0])
    if k % 512:
        return np.exp2(np.random.permutation(np.resize(levels, k // 32))).repeat(32)
    a = np.empty((k // 512, 16))
    for p in range(k // 512):
        a[p, :8] = np.random.permutation(np.resize(levels, 8))
        for g in range(8):
            far = levels[np.abs(levels - a[p, g]) >= 10]
            a[p, g + 8] = far[np.random.randint(len(far))]
    return np.exp2(a.ravel()).repeat(32)


BF16 = ml_dtypes.bfloat16


def bf(x):
    return np.asarray(x, np.float32).astype(BF16)


def f64(x):
    return np.asarray(x).astype(np.float64)


B, G, C, F, NC = 8, 16, 512, 128, 4096
HW = G * G
KS = 3
P_GEM = 3.0
EPS_GEM = 1e-6
EPS_NORM = 1e-12


def l2n(v, axis):
    n = np.sqrt(np.sum(v * v, axis=axis, keepdims=True))
    return v / np.maximum(n, EPS_NORM)


def erf(v):
    a = np.clip(v, -7.0, 7.0)
    a2 = 2.0 * a * a
    term = a.copy()
    tot = a.copy()
    for n in range(1, 140):
        term = term * a2 / (2 * n + 1)
        tot = tot + term
    return 2.0 / np.sqrt(np.pi) * np.exp(-a * a) * tot


def gelu_erf(v):
    return 0.5 * v * (1.0 + erf(v / np.sqrt(2.0)))


def setup_inputs():
    s = mx_kscale(C)
    t = s / s.min()
    g = 2.0 ** np.round(0.5 * np.log2(np.mean(t * t)))
    return {"patch_tokens": bf(np.random.standard_normal((B, HW, C)) * 2.0 / G * t),
            "fc1_w": bf(np.random.standard_normal((C, F)) * (g / t)[:, None]),
            "fc1_b": bf(np.random.standard_normal(F) * 0.3)}


def reference(patch_tokens, fc1_w, fc1_b):
    x = f64(patch_tokens)
    padded = np.pad(x.reshape(B, G, G, C), ((0, 0), (KS - 1, 0), (KS // 2, KS // 2), (0, 0)))
    acc = np.zeros_like(x)
    for ki in range(KS):
        for kj in range(KS):
            y = padded[:, ki:ki + G, kj:kj + G, :].reshape(B, HW, C)
            acc = acc + np.maximum(l2n(x * y, 1), EPS_GEM) ** P_GEM
    pooled = (acc / (KS * KS)) ** (1.0 / P_GEM)
    tokens = l2n(pooled + x, 2)
    return gelu_erf((mxq(tokens, 2, "e4m3") @ mxq(f64(fc1_w), 0, "e4m3")) + f64(fc1_b))

@@ -1,0 +1,417 @@
+from contextlib import ExitStack
+
+import concourse.mybir as mybir
+from concourse.masks import make_identity
+
+F32 = mybir.dt.float32
+BF16 = mybir.dt.bfloat16
+U32 = mybir.dt.uint32
+U8 = mybir.dt.uint8
+FP8X4 = mybir.dt.float8_e4m3fn_x4
+ALU = mybir.AluOpType
+ACT = mybir.ActivationFunctionType
+
+P = 128
+B = 8
+GRID = 16
+T = GRID * GRID
+H = T // P
+C = 512
+CH = C // P
+F = 128
+PACK = 4
+
+FLOPS = 2 * B * T * C * F
+
+OFFSETS = [(0, 0), (0, -1), (-1, -1), (-1, 0), (-1, 1), (-2, -1), (-2, 0), (-2, 1)]
+K = len(OFFSETS)
+K_LEFT = OFFSETS.index((0, -1))
+TERMS = [(k, 0) for k in range(K)] + [(K_LEFT, 1)]
+
+MAX_TOP = 2
+PADDED = GRID + 2
+TERM_COLS = T + 4
+
+EPS_GEM_CUBED = 1e-18
+EPS_NORM_SQUARED = 1e-24
+
+PAIR = 2
+ROUND = 2
+CLOSING_STEPS = 8
+
+
+def tile_tokenmudule_pa_s_kernel(tc, patch_tokens, fc1_w, fc1_b, out):
+    nc = tc.nc
+
+    with ExitStack() as ctx:
+        ctx.enter_context(tc.manual_schedule())
+
+        def sbuf(name, bufs):
+            return ctx.enter_context(tc.tile_pool(name=name, bufs=bufs))
+
+        def psum(name, bufs):
+            return ctx.enter_context(tc.psum_pool(name=name, bufs=bufs))
+
+        keep = sbuf("keep", 1)
+        unread_pool = sbuf("unread", 4)
+        coef_pool = sbuf("coef", 2)
+        pooled_pool = sbuf("pooled", 2 * ROUND)
+        tail_pool = sbuf("tail", ROUND)
+        xT_psum = psum("xT_psum", 2)
+        acc_psum = psum("acc_psum", ROUND * H)
+        proj_psum = psum("proj_psum", 2)
+
+        x_nat = keep.tile([P, B, H, C], BF16)
+        for b in range(B):
+            nc.sync.dma_start(
+                out=x_nat[:, b], in_=patch_tokens[b].rearrange("(h p) c -> p h c", p=P)
+            )
+        w_raw = keep.tile([P, PACK, F], BF16)
+        nc.scalar.dma_start(out=w_raw[:], in_=fc1_w.rearrange("(p t) f -> p t f", t=PACK))
+        bias = keep.tile([P, F], BF16)
+        nc.scalar.dma_start(out=bias[:], in_=fc1_b.partition_broadcast(P))
+
+        ident_bf = keep.tile([P, P], BF16)
+        make_identity(nc, ident_bf[:])
+        ident_f = keep.tile([P, P], F32)
+        make_identity(nc, ident_f[:])
+        plus_eps = keep.tile([P, 1], F32)
+        nc.vector.memset(plus_eps[:], EPS_GEM_CUBED)
+        minus_eps = keep.tile([P, 1], F32)
+        nc.vector.memset(minus_eps[:], -EPS_GEM_CUBED)
+
+        q_pad = keep.tile([P, B, CH, GRID, PADDED], F32)
+        p_pad = keep.tile([P, 2, CH, GRID, PADDED], F32)
+        for padded in (q_pad, p_pad):
+            rows = padded[:].rearrange("p b c i j -> p (b c i) j")
+            nc.vector.memset(rows[:, :, 0:2], 0.0)
+            nc.vector.memset(rows[:, :, PADDED - 2 : PADDED], 0.0)
+        term_tiles = [
+            keep.tile([P, K, PAIR, TERM_COLS], F32, name="terms%d" % i) for i in range(3)
+        ]
+        for terms in term_tiles:
+            nc.vector.memset(terms[:, :, :, T - 1 : TERM_COLS], 0.0)
+            nc.vector.memset(terms[:, :, :, 0 : MAX_TOP * GRID], 0.0)
+
+        w_grouped = keep.tile([P, F, PACK], BF16, align_bytes=64)
+        w_codes = keep.tile([P, F], U32, align_bytes=64)
+        w_scales = keep.tile([P, F], U8, align_bytes=64)
+        nc.vector.tensor_copy(out=w_grouped[:], in_=w_raw[:].rearrange("p t f -> p f t"))
+        nc.vector.quantize_mx(
+            out=w_codes[:].bitcast(FP8X4),
+            scales=w_scales[:],
+            in_=w_grouped[:].rearrange("p f t -> p (f t)"),
+        )
+
+        own_sq = keep.tile([P, B, CH], F32)
+        pre_act = keep.tile([P, B, H, F], F32)
+        result = keep.tile([P, B, H, F], F32)
+
+        xT = {}
+        norm_sq = {}
+        norm = {}
+        inv_norm = {}
+        coef = {}
+        acc = {}
+        pooled = {}
+        closing = {}
+        steps_done = {}
+
+        def grid(ap):
+            return ap.rearrange("p (i j) -> p i j", j=GRID)
+
+        def shifted(padded, top, dj):
+            return padded[:, 0 : GRID - top, 1 + dj : 1 + dj + GRID]
+
+        def transpose_x(b):
+            xT[b] = xT_psum.tile([P, CH, T], BF16, name="xT")
+            for h in range(H):
+                for ch in range(CH):
+                    nc.tensor.transpose(
+                        xT[b][:, ch, h * P : (h + 1) * P],
+                        x_nat[:, b, h, ch * P : (ch + 1) * P],
+                        ident_bf[:],
+                    )
+
+        def square_x(b):
+            transpose_x(b)
+            q = q_pad[:, b]
+            nc.scalar.activation(
+                out=q[:, :, :, 1 : 1 + GRID],
+                in_=xT[b][:].rearrange("p c (i j) -> p c i j", j=GRID),
+                func=ACT.Square,
+            )
+            for ch in range(CH):
+                unread = unread_pool.tile([P, GRID, PADDED], BF16, name="unread_s")
+                nc.scalar.activation(
+                    out=unread[:],
+                    in_=q[:, ch],
+                    func=ACT.Square,
+                    accum_out=own_sq[:, b, ch : ch + 1],
+                )
+
+        def sum_products(b, k):
+            if k == 1:
+                norm_sq[b] = coef_pool.tile([P, K, CH], F32, name="norm_sq")
+            di, dj = OFFSETS[k]
+            top = -di
+            q = q_pad[:, b]
+            for ch in range(CH):
+                unread = unread_pool.tile([P, GRID, GRID], F32, name="unread_v")
+                nc.vector.scalar_tensor_tensor(
+                    out=unread[:, top:GRID, :],
+                    in0=q[:, ch, top:GRID, 1 : 1 + GRID],
+                    scalar=1.0,
+                    in1=shifted(q[:, ch], top, dj),
+                    op0=ALU.mult,
+                    op1=ALU.mult,
+                    accum_out=norm_sq[b][:, k, ch : ch + 1],
+                )
+
+        def start_coefficients(b):
+            floored = coef_pool.tile([P, K, CH], F32, name="n_floored")
+            nc.vector.tensor_scalar_max(floored[:, 0, :], own_sq[:, b, :], EPS_NORM_SQUARED)
+            nc.vector.tensor_scalar_max(floored[:, 1:K, :], norm_sq[b][:, 1:K, :], EPS_NORM_SQUARED)
+            norm[b] = coef_pool.tile([P, K, CH], F32, name="norm")
+            nc.scalar.activation(out=norm[b][:], in_=floored[:], func=ACT.Sqrt)
+
+        def finish_coefficients(b):
+            inv_norm[b] = coef_pool.tile([P, K, CH], F32, name="inv_norm")
+            nc.vector.reciprocal(inv_norm[b][:], norm[b][:])
+            ratio = coef_pool.tile([P, K, CH], F32, name="ratio")
+            nc.vector.tensor_tensor(
+                out=ratio[:],
+                in0=inv_norm[b][:],
+                in1=norm[b][:, 0:1, :].to_broadcast([P, K, CH]),
+                op=ALU.mult,
+            )
+            ratio_sq = coef_pool.tile([P, K, CH], F32, name="ratio_sq")
+            nc.vector.tensor_tensor(out=ratio_sq[:], in0=ratio[:], in1=ratio[:], op=ALU.mult)
+            coef[b] = coef_pool.tile([P, K, CH], F32, name="coef")
+            nc.vector.tensor_tensor(
+                out=coef[b][:], in0=ratio_sq[:], in1=inv_norm[b][:], op=ALU.mult
+            )
+
+        def scale_cubes(b):
+            for ch in range(CH):
+                nc.vector.scalar_tensor_tensor(
+                    out=p_pad[:, b % 2, ch, :, 1 : 1 + GRID],
+                    in0=q_pad[:, b, ch, :, 1 : 1 + GRID],
+                    scalar=inv_norm[b][:, 0, ch : ch + 1],
+                    in1=grid(xT[b][:, ch, :]),
+                    op0=ALU.mult,
+                    op1=ALU.mult,
+                )
+
+        def window_terms(b, pair):
+            terms = term_tiles[(b * (CH // PAIR) + pair) % 3]
+            chunks = slice(pair * PAIR, (pair + 1) * PAIR)
+            p = p_pad[:, b % 2]
+            for k in range(K):
+                di, dj = OFFSETS[k]
+                top = -di
+                products = terms[:, k, :, top * GRID : T].rearrange("p c (i j) -> p c i j", j=GRID)
+                if k == 0:
+                    nc.scalar.activation(
+                        out=products, in_=p[:, chunks, :, 1 : 1 + GRID], func=ACT.Square
+                    )
+                else:
+                    nc.vector.tensor_tensor(
+                        out=products,
+                        in0=p[:, chunks, top:GRID, 1 : 1 + GRID],
+                        in1=p[:, chunks, 0 : GRID - top, 1 + dj : 1 + dj + GRID],
+                        op=ALU.mult,
+                    )
+                for c in range(PAIR):
+                    nc.scalar.activation(
+                        out=terms[:, k, c, top * GRID : T],
+                        in_=terms[:, k, c, top * GRID : T],
+                        func=ACT.Relu,
+                        scale=coef[b][:, k, pair * PAIR + c : pair * PAIR + c + 1],
+                        bias=minus_eps[:],
+                    )
+
+        def window_sum(b, pair):
+            terms = term_tiles[(b * (CH // PAIR) + pair) % 3]
+            if pair == 0:
+                for h in range(H):
+                    acc[b, h] = acc_psum.tile([P, C], F32, name="acc")
+            for c in range(PAIR):
+                ch = pair * PAIR + c
+                for i, (k, ahead) in enumerate(TERMS):
+                    for h in range(H):
+                        nc.tensor.matmul(
+                            acc[b, h][:, ch * P : (ch + 1) * P],
+                            lhsT=terms[:, k, c, ahead + h * P : ahead + (h + 1) * P],
+                            rhs=ident_f[:],
+                            is_transpose=True,
+                            start=(i == 0),
+                            stop=(i == len(TERMS) - 1),
+                        )
+
+        def square_sum(on_vector, values, unread, total):
+            if on_vector:
+                nc.vector.scalar_tensor_tensor(
+                    out=unread,
+                    in0=values,
+                    scalar=1.0,
+                    in1=values,
+                    op0=ALU.mult,
+                    op1=ALU.mult,
+                    accum_out=total,
+                )
+            else:
+                nc.scalar.activation(out=unread, in_=values, func=ACT.Square, accum_out=total)
+
+        def scale_rows(on_vector, scaled, values, factor):
+            if on_vector:
+                nc.vector.tensor_scalar_mul(scaled, values, factor)
+            else:
+                nc.scalar.activation(out=scaled, in_=values, func=ACT.Copy, scale=factor)
+
+        def copy_from_psum(on_vector, copied, values):
+            if on_vector:
+                nc.vector.tensor_copy(out=copied, in_=values)
+            else:
+                nc.scalar.copy(out=copied, in_=values)
+
+        def close_round(first, on_vector):
+            step = steps_done.get(first, 0)
+            steps_done[first] = step + 1
+            images = range(first, first + ROUND)
+            if step == 0:
+                for b in images:
+                    pooled[b] = pooled_pool.tile([P, H, C], F32, name="pooled")
+                    for h in range(H):
+                        nc.scalar.activation(
+                            out=pooled[b][:, h, :],
+                            in_=acc[b, h][:],
+                            func=ACT.Ln,
+                            scale=1.0 / len(TERMS),
+                            bias=plus_eps[:],
+                        )
+            elif step == 1:
+                for b in images:
+                    nc.scalar.activation(
+                        out=pooled[b][:], in_=pooled[b][:], func=ACT.Exp, scale=1.0 / 3.0
+                    )
+            elif step == 2:
+                for b in images:
+                    nc.vector.tensor_tensor(
+                        out=pooled[b][:], in0=pooled[b][:], in1=x_nat[:, b], op=ALU.add
+                    )
+            elif step == 3:
+                r_sq = tail_pool.tile([P, ROUND, H], F32, name="r_sq")
+                closing[first, "r_sq"] = r_sq
+                for b in images:
+                    unread = tail_pool.tile([P, H, C], F32, name="unread_r")
+                    for h in range(H):
+                        square_sum(
+                            on_vector,
+                            pooled[b][:, h, :],
+                            unread[:, h, :],
+                            r_sq[:, b - first, h : h + 1],
+                        )
+            elif step == 4:
+                floored = tail_pool.tile([P, ROUND, H], F32, name="r_floored")
+                nc.vector.tensor_scalar_max(floored[:], closing[first, "r_sq"][:], EPS_NORM_SQUARED)
+                r_norm = tail_pool.tile([P, ROUND, H], F32, name="r_norm")
+                closing[first, "r_norm"] = r_norm
+                nc.scalar.activation(out=r_norm[:], in_=floored[:], func=ACT.Sqrt)
+            elif step == 5:
+                inv_r = tail_pool.tile([P, ROUND, H], F32, name="inv_r")
+                nc.vector.reciprocal(inv_r[:], closing[first, "r_norm"][:])
+                for b in images:
+                    tokens = tail_pool.tile([P, H, C], BF16, name="tokens")
+                    closing[b, "tokens"] = tokens
+                    for h in range(H):
+                        scale_rows(
+                            on_vector,
+                            tokens[:, h, :],
+                            pooled[b][:, h, :],
+                            inv_r[:, b - first, h : h + 1],
+                        )
+                for b in images:
+                    tokens = closing[b, "tokens"]
+                    words = tokens[:].rearrange("p h c -> p (h c)").bitcast(F32)
+                    tokT = proj_psum.tile([P, H, 2, P], F32, name="proj")
+                    for h in range(H):
+                        for u in range(2):
+                            nc.tensor.transpose(
+                                tokT[:, h, u, :],
+                                words[:, h * (C // 2) + u : (h + 1) * (C // 2) : 2],
+                                ident_f[:],
+                            )
+                    grouped = tail_pool.tile([P, H * P * PACK], BF16, name="grouped", align_bytes=64)
+                    closing[b, "grouped"] = grouped
+                    copy_from_psum(
+                        on_vector,
+                        grouped[:].bitcast(F32).rearrange("p (h r u) -> p h r u", h=H, u=2),
+                        tokT[:].rearrange("p h u r -> p h r u"),
+                    )
+            elif step == 6:
+                for b in images:
+                    codes = tail_pool.tile([P, H * P], U32, name="codes", align_bytes=64)
+                    scales = tail_pool.tile([P, H * P], U8, name="scales", align_bytes=64)
+                    nc.vector.quantize_mx(
+                        out=codes[:].bitcast(FP8X4),
+                        scales=scales[:],
+                        in_=closing[b, "grouped"][:],
+                    )
+                    product = proj_psum.tile([P, H, F], F32, name="proj")
+                    closing[b, "product"] = product
+                    for h in range(H):
+                        nc.tensor.matmul_mx(
+                            out=product[:, h, :],
+                            lhsT=codes[:, h * P : (h + 1) * P].bitcast(FP8X4),
+                            lhsT_scale=scales[:, h * P : (h + 1) * P],
+                            rhs=w_codes[:].bitcast(FP8X4),
+                            rhs_scale=w_scales[:],
+                            start=True,
+                            stop=True,
+                        )
+            else:
+                for b in images:
+                    nc.vector.tensor_tensor(
+                        out=pre_act[:, b],
+                        in0=closing[b, "product"][:],
+                        in1=bias[:].unsqueeze(1).to_broadcast([P, H, F]),
+                        op=ALU.add,
+                    )
+
+        for b in range(2):
+            for i in range(B // 2):
+                square_x(b * (B // 2) + i)
+            for k in range(1, K):
+                sum_products(b, k)
+            start_coefficients(b)
+        transpose_x(0)
+        finish_coefficients(0)
+        scale_cubes(0)
+
+        for b in range(B):
+            if b + 1 < B:
+                transpose_x(b + 1)
+            for pair in range(CH // PAIR):
+                window_terms(b, pair)
+                window_sum(b, pair)
+            if b + 1 < B:
+                finish_coefficients(b + 1)
+                scale_cubes(b + 1)
+            if b + 2 < B:
+                for k in range(1, K):
+                    sum_products(b + 2, k)
+                    if k % 2 == 0:
+                        for first in range(0, b, ROUND):
+                            if steps_done.get(first, 0) < CLOSING_STEPS:
+                                close_round(first, False)
+                start_coefficients(b + 2)
+        for first in range(0, B, ROUND):
+            while steps_done.get(first, 0) < CLOSING_STEPS:
+                close_round(first, True)
+
+        stored = out.rearrange("b (h p) f -> p b h f", p=P)
+        for first in range(0, B, ROUND):
+            images = slice(first, first + ROUND)
+            nc.scalar.activation(out=result[:, images], in_=pre_act[:, images], func=ACT.Gelu)
+            nc.sync.dma_start(out=stored[:, images], in_=result[:, images])

@@ -29,8 +29,10 @@ K_LEFT = OFFSETS.index((0, -1))
 TERMS = [(k, 0) for k in range(K)] + [(K_LEFT, 1)]
 
 MAX_TOP = 2
-PADDED = GRID + 2
-TERM_COLS = T + 4
+LEAD = 4
+ROW = LEAD + GRID
+PADDED = GRID * ROW + 8
+TERM_COLS = T + 8
 
 EPS_GEM_CUBED = 1e-18
 EPS_NORM_SQUARED = 1e-24
@@ -80,18 +82,15 @@ def tile_tokenmudule_pa_s_kernel(tc, patch_tokens, fc1_w, fc1_b, out):
         minus_eps = keep.tile([P, 1], F32)
         nc.vector.memset(minus_eps[:], -EPS_GEM_CUBED)
 
-        q_pad = keep.tile([P, B, CH, GRID, PADDED], F32)
-        p_pad = keep.tile([P, 2, CH, GRID, PADDED], F32)
-        for padded in (q_pad, p_pad):
-            rows = padded[:].rearrange("p b c i j -> p (b c i) j")
-            nc.vector.memset(rows[:, :, 0:2], 0.0)
-            nc.vector.memset(rows[:, :, PADDED - 2 : PADDED], 0.0)
+        q = keep.tile([P, B, CH, T], F32)
+        p_pad = keep.tile([P, 2, CH, PADDED], F32)
+        nc.gpsimd.memset(p_pad[:], 0.0)
         term_tiles = [
             keep.tile([P, K, PAIR, TERM_COLS], F32, name="terms%d" % i) for i in range(3)
         ]
         for terms in term_tiles:
-            nc.vector.memset(terms[:, :, :, T - 1 : TERM_COLS], 0.0)
-            nc.vector.memset(terms[:, :, :, 0 : MAX_TOP * GRID], 0.0)
+            nc.gpsimd.memset(terms[:, K_LEFT, :, T:TERM_COLS], 0.0)
+            nc.gpsimd.memset(terms[:, :, :, 0 : MAX_TOP * GRID], 0.0)
 
         w_grouped = keep.tile([P, F, PACK], BF16, align_bytes=64)
         w_codes = keep.tile([P, F], U32, align_bytes=64)
@@ -120,8 +119,10 @@ def tile_tokenmudule_pa_s_kernel(tc, patch_tokens, fc1_w, fc1_b, out):
         def grid(ap):
             return ap.rearrange("p (i j) -> p i j", j=GRID)
 
-        def shifted(padded, top, dj):
-            return padded[:, 0 : GRID - top, 1 + dj : 1 + dj + GRID]
+        def padded_rows(b, chunks, dj):
+            first = LEAD + dj
+            flat = p_pad[:, b % 2, chunks, first : first + GRID * ROW]
+            return flat.rearrange("p c (i j) -> p c i j", j=ROW)[:, :, :, 0:GRID]
 
         def transpose_x(b):
             xT[b] = xT_psum.tile([P, CH, T], BF16, name="xT")
@@ -135,17 +136,12 @@ def tile_tokenmudule_pa_s_kernel(tc, patch_tokens, fc1_w, fc1_b, out):
 
         def square_x(b):
             transpose_x(b)
-            q = q_pad[:, b]
-            nc.scalar.activation(
-                out=q[:, :, :, 1 : 1 + GRID],
-                in_=xT[b][:].rearrange("p c (i j) -> p c i j", j=GRID),
-                func=ACT.Square,
-            )
+            nc.scalar.activation(out=q[:, b], in_=xT[b][:], func=ACT.Square)
             for ch in range(CH):
-                unread = unread_pool.tile([P, GRID, PADDED], BF16, name="unread_s")
+                unread = unread_pool.tile([P, T], BF16, name="unread_s")
                 nc.scalar.activation(
                     out=unread[:],
-                    in_=q[:, ch],
+                    in_=q[:, b, ch],
                     func=ACT.Square,
                     accum_out=own_sq[:, b, ch : ch + 1],
                 )
@@ -155,14 +151,15 @@ def tile_tokenmudule_pa_s_kernel(tc, patch_tokens, fc1_w, fc1_b, out):
                 norm_sq[b] = coef_pool.tile([P, K, CH], F32, name="norm_sq")
             di, dj = OFFSETS[k]
             top = -di
-            q = q_pad[:, b]
+            lo, hi = max(0, -dj), GRID - max(0, dj)
+            rows, cols = GRID - top, hi - lo
             for ch in range(CH):
-                unread = unread_pool.tile([P, GRID, GRID], F32, name="unread_v")
+                unread = unread_pool.tile([P, T], F32, name="unread_v")
                 nc.vector.scalar_tensor_tensor(
-                    out=unread[:, top:GRID, :],
-                    in0=q[:, ch, top:GRID, 1 : 1 + GRID],
+                    out=unread[:, 0 : rows * cols].rearrange("p (i j) -> p i j", j=cols),
+                    in0=grid(q[:, b, ch, :])[:, top:GRID, lo:hi],
                     scalar=1.0,
-                    in1=shifted(q[:, ch], top, dj),
+                    in1=grid(q[:, b, ch, :])[:, 0:rows, lo + dj : hi + dj],
                     op0=ALU.mult,
                     op1=ALU.mult,
                     accum_out=norm_sq[b][:, k, ch : ch + 1],
@@ -195,8 +192,8 @@ def tile_tokenmudule_pa_s_kernel(tc, patch_tokens, fc1_w, fc1_b, out):
         def scale_cubes(b):
             for ch in range(CH):
                 nc.vector.scalar_tensor_tensor(
-                    out=p_pad[:, b % 2, ch, :, 1 : 1 + GRID],
-                    in0=q_pad[:, b, ch, :, 1 : 1 + GRID],
+                    out=padded_rows(b, slice(ch, ch + 1), 0)[:, 0],
+                    in0=grid(q[:, b, ch, :]),
                     scalar=inv_norm[b][:, 0, ch : ch + 1],
                     in1=grid(xT[b][:, ch, :]),
                     op0=ALU.mult,
@@ -206,20 +203,19 @@ def tile_tokenmudule_pa_s_kernel(tc, patch_tokens, fc1_w, fc1_b, out):
         def window_terms(b, pair):
             terms = term_tiles[(b * (CH // PAIR) + pair) % 3]
             chunks = slice(pair * PAIR, (pair + 1) * PAIR)
-            p = p_pad[:, b % 2]
             for k in range(K):
                 di, dj = OFFSETS[k]
                 top = -di
                 products = terms[:, k, :, top * GRID : T].rearrange("p c (i j) -> p c i j", j=GRID)
                 if k == 0:
                     nc.scalar.activation(
-                        out=products, in_=p[:, chunks, :, 1 : 1 + GRID], func=ACT.Square
+                        out=products, in_=padded_rows(b, chunks, 0), func=ACT.Square
                     )
                 else:
                     nc.vector.tensor_tensor(
                         out=products,
-                        in0=p[:, chunks, top:GRID, 1 : 1 + GRID],
-                        in1=p[:, chunks, 0 : GRID - top, 1 + dj : 1 + dj + GRID],
+                        in0=padded_rows(b, chunks, 0)[:, :, top:GRID, :],
+                        in1=padded_rows(b, chunks, dj)[:, :, 0 : GRID - top, :],
                         op=ALU.mult,
                     )
                 for c in range(PAIR):

@@ -23,8 +23,12 @@ PACK = 4
 
 FLOPS = 2 * B * T * C * F
 
-OFFSETS = [(0, 0), (0, -1), (-1, -1), (-1, 0), (-1, 1), (-2, -1), (-2, 0), (-2, 1)]
+OFFSETS = [(0, -1), (-1, 0), (-1, -1), (-1, 1), (-2, -1), (-2, 0), (-2, 1), (0, 0)]
 K = len(OFFSETS)
+OWN = OFFSETS.index((0, 0))
+ON_V = 3
+V_CLAMPS = 3
+V_CLAMPS_LAST = 4
 K_LEFT = OFFSETS.index((0, -1))
 TERMS = [(k, 0) for k in range(K)] + [(K_LEFT, 1)]
 
@@ -37,9 +41,10 @@ TERM_COLS = T + 8
 EPS_GEM_CUBED = 1e-18
 EPS_NORM_SQUARED = 1e-24
 
+TERM_TILES = 5
 PAIR = 2
+ROUNDS = [(0, 1), (2, 3), (4, 5), (6,), (7,)]
 ROUND = 2
-CLOSING_STEPS = 8
 
 
 def tile_tokenmudule_pa_s_kernel(tc, patch_tokens, fc1_w, fc1_b, out):
@@ -55,13 +60,16 @@ def tile_tokenmudule_pa_s_kernel(tc, patch_tokens, fc1_w, fc1_b, out):
             return ctx.enter_context(tc.psum_pool(name=name, bufs=bufs))
 
         keep = sbuf("keep", 1)
+        nat_pool = sbuf("nat", 2)
+        q_pool = sbuf("q", 3)
         unread_pool = sbuf("unread", 4)
-        coef_pool = sbuf("coef", 2)
+        coef_pool = sbuf("coef", 3)
         pooled_pool = sbuf("pooled", 2 * ROUND)
-        tail_pool = sbuf("tail", ROUND)
-        xT_psum = psum("xT_psum", 2)
+        tail_pool = sbuf("tail", 2 * ROUND)
+        xT_psum = psum("xT_psum", 1)
+        qT_psum = psum("qT_psum", CH // PAIR)
         acc_psum = psum("acc_psum", ROUND * H)
-        proj_psum = psum("proj_psum", 2)
+        proj_psum = psum("proj_psum", 1)
 
         x_nat = keep.tile([P, B, H, C], BF16)
         for b in range(B):
@@ -82,15 +90,14 @@ def tile_tokenmudule_pa_s_kernel(tc, patch_tokens, fc1_w, fc1_b, out):
         minus_eps = keep.tile([P, 1], F32)
         nc.vector.memset(minus_eps[:], -EPS_GEM_CUBED)
 
-        q = keep.tile([P, B, CH, T], F32)
         p_pad = keep.tile([P, 2, CH, PADDED], F32)
         nc.gpsimd.memset(p_pad[:], 0.0)
         term_tiles = [
-            keep.tile([P, K, PAIR, TERM_COLS], F32, name="terms%d" % i) for i in range(3)
+            keep.tile([P, K, PAIR, TERM_COLS], F32, name="terms%d" % i) for i in range(TERM_TILES)
         ]
         for terms in term_tiles:
             nc.gpsimd.memset(terms[:, K_LEFT, :, T:TERM_COLS], 0.0)
-            nc.gpsimd.memset(terms[:, :, :, 0 : MAX_TOP * GRID], 0.0)
+            nc.gpsimd.memset(terms[:, 0:OWN, :, 0 : MAX_TOP * GRID], 0.0)
 
         w_grouped = keep.tile([P, F, PACK], BF16, align_bytes=64)
         w_codes = keep.tile([P, F], U32, align_bytes=64)
@@ -102,11 +109,16 @@ def tile_tokenmudule_pa_s_kernel(tc, patch_tokens, fc1_w, fc1_b, out):
             in_=w_grouped[:].rearrange("p f t -> p (f t)"),
         )
 
+        scratch = keep.tile([P, 1], F32)
+        nc.vector.memset(scratch[:], 1.0)
         own_sq = keep.tile([P, B, CH], F32)
         pre_act = keep.tile([P, B, H, F], F32)
         result = keep.tile([P, B, H, F], F32)
 
         xT = {}
+        q_nat = {}
+        qT = {}
+        q = {}
         norm_sq = {}
         norm = {}
         inv_norm = {}
@@ -114,7 +126,6 @@ def tile_tokenmudule_pa_s_kernel(tc, patch_tokens, fc1_w, fc1_b, out):
         acc = {}
         pooled = {}
         closing = {}
-        steps_done = {}
 
         def grid(ap):
             return ap.rearrange("p (i j) -> p i j", j=GRID)
@@ -134,32 +145,58 @@ def tile_tokenmudule_pa_s_kernel(tc, patch_tokens, fc1_w, fc1_b, out):
                         ident_bf[:],
                     )
 
-        def square_x(b):
-            transpose_x(b)
-            nc.scalar.activation(out=q[:, b], in_=xT[b][:], func=ACT.Square)
-            for ch in range(CH):
+        def square_x(b, pieces=1):
+            q_nat[b] = nat_pool.tile([P, H, C], F32, name="q_nat")
+            for i in range(pieces):
+                cols = slice(i * C // pieces, (i + 1) * C // pieces)
+                nc.scalar.activation(
+                    out=q_nat[b][:, :, cols], in_=x_nat[:, b, :, cols], func=ACT.Square
+                )
+
+        def transpose_q(b, half):
+            qT[b, half] = qT_psum.tile([P, PAIR, T], F32, name="qT")
+            for c in range(PAIR):
+                ch = half * PAIR + c
+                for h in range(H):
+                    nc.tensor.transpose(
+                        qT[b, half][:, c, h * P : (h + 1) * P],
+                        q_nat[b][:, h, ch * P : (ch + 1) * P],
+                        ident_f[:],
+                    )
+
+        def copy_q(b, half, on_vector=False):
+            if half == 0:
+                q[b] = q_pool.tile([P, CH, T], F32, name="q")
+            copied = q[b][:, half * PAIR : (half + 1) * PAIR, :]
+            if on_vector:
+                nc.vector.tensor_copy(out=copied, in_=qT[b, half][:])
+            else:
+                nc.scalar.copy(out=copied, in_=qT[b, half][:])
+
+        def sum_squares(b, half):
+            for ch in range(half * PAIR, (half + 1) * PAIR):
                 unread = unread_pool.tile([P, T], BF16, name="unread_s")
                 nc.scalar.activation(
                     out=unread[:],
-                    in_=q[:, b, ch],
+                    in_=q[b][:, ch],
                     func=ACT.Square,
                     accum_out=own_sq[:, b, ch : ch + 1],
                 )
 
-        def sum_products(b, k):
-            if k == 1:
+        def sum_products(b, k, half):
+            if b not in norm_sq:
                 norm_sq[b] = coef_pool.tile([P, K, CH], F32, name="norm_sq")
             di, dj = OFFSETS[k]
             top = -di
             lo, hi = max(0, -dj), GRID - max(0, dj)
             rows, cols = GRID - top, hi - lo
-            for ch in range(CH):
+            for ch in range(half * PAIR, (half + 1) * PAIR):
                 unread = unread_pool.tile([P, T], F32, name="unread_v")
                 nc.vector.scalar_tensor_tensor(
                     out=unread[:, 0 : rows * cols].rearrange("p (i j) -> p i j", j=cols),
-                    in0=grid(q[:, b, ch, :])[:, top:GRID, lo:hi],
+                    in0=grid(qT[b, half][:, ch % PAIR, :])[:, top:GRID, lo:hi],
                     scalar=1.0,
-                    in1=grid(q[:, b, ch, :])[:, 0:rows, lo + dj : hi + dj],
+                    in1=grid(q[b][:, ch, :])[:, 0:rows, lo + dj : hi + dj],
                     op0=ALU.mult,
                     op1=ALU.mult,
                     accum_out=norm_sq[b][:, k, ch : ch + 1],
@@ -167,68 +204,109 @@ def tile_tokenmudule_pa_s_kernel(tc, patch_tokens, fc1_w, fc1_b, out):
 
         def start_coefficients(b):
             floored = coef_pool.tile([P, K, CH], F32, name="n_floored")
-            nc.vector.tensor_scalar_max(floored[:, 0, :], own_sq[:, b, :], EPS_NORM_SQUARED)
-            nc.vector.tensor_scalar_max(floored[:, 1:K, :], norm_sq[b][:, 1:K, :], EPS_NORM_SQUARED)
+            nc.vector.tensor_scalar_max(floored[:, OWN, :], own_sq[:, b, :], EPS_NORM_SQUARED)
+            nc.vector.tensor_scalar_max(
+                floored[:, 0:OWN, :], norm_sq[b][:, 0:OWN, :], EPS_NORM_SQUARED
+            )
             norm[b] = coef_pool.tile([P, K, CH], F32, name="norm")
             nc.scalar.activation(out=norm[b][:], in_=floored[:], func=ACT.Sqrt)
 
-        def finish_coefficients(b):
+        def coefficient_steps(b):
             inv_norm[b] = coef_pool.tile([P, K, CH], F32, name="inv_norm")
-            nc.vector.reciprocal(inv_norm[b][:], norm[b][:])
             ratio = coef_pool.tile([P, K, CH], F32, name="ratio")
-            nc.vector.tensor_tensor(
-                out=ratio[:],
-                in0=inv_norm[b][:],
-                in1=norm[b][:, 0:1, :].to_broadcast([P, K, CH]),
-                op=ALU.mult,
-            )
             ratio_sq = coef_pool.tile([P, K, CH], F32, name="ratio_sq")
-            nc.vector.tensor_tensor(out=ratio_sq[:], in0=ratio[:], in1=ratio[:], op=ALU.mult)
             coef[b] = coef_pool.tile([P, K, CH], F32, name="coef")
-            nc.vector.tensor_tensor(
-                out=coef[b][:], in0=ratio_sq[:], in1=inv_norm[b][:], op=ALU.mult
-            )
+            return [
+                lambda: nc.vector.reciprocal(inv_norm[b][:], norm[b][:]),
+                lambda: nc.vector.tensor_tensor(
+                    out=ratio[:],
+                    in0=inv_norm[b][:],
+                    in1=norm[b][:, OWN : OWN + 1, :].to_broadcast([P, K, CH]),
+                    op=ALU.mult,
+                ),
+                lambda: nc.vector.tensor_tensor(
+                    out=ratio_sq[:], in0=ratio[:], in1=ratio[:], op=ALU.mult
+                ),
+                lambda: nc.vector.tensor_tensor(
+                    out=coef[b][:], in0=ratio_sq[:], in1=inv_norm[b][:], op=ALU.mult
+                ),
+            ]
 
-        def scale_cubes(b):
-            for ch in range(CH):
+        def scale_cubes(b, pair):
+            for ch in range(pair * PAIR, (pair + 1) * PAIR):
                 nc.vector.scalar_tensor_tensor(
                     out=padded_rows(b, slice(ch, ch + 1), 0)[:, 0],
-                    in0=grid(q[:, b, ch, :]),
-                    scalar=inv_norm[b][:, 0, ch : ch + 1],
+                    in0=grid(q[b][:, ch, :]),
+                    scalar=inv_norm[b][:, OWN, ch : ch + 1],
                     in1=grid(xT[b][:, ch, :]),
                     op0=ALU.mult,
                     op1=ALU.mult,
                 )
 
-        def window_terms(b, pair):
-            terms = term_tiles[(b * (CH // PAIR) + pair) % 3]
+        def terms_of(b, pair):
+            return term_tiles[(b * (CH // PAIR) + pair) % TERM_TILES]
+
+        def products_of(b, pair, k):
+            top = -OFFSETS[k][0]
+            return terms_of(b, pair)[:, k, :, top * GRID : T].rearrange(
+                "p c (i j) -> p c i j", j=GRID
+            )
+
+        def on_vector_count(b):
+            return OWN if b == B - 1 else ON_V
+
+        def multiply(b, pair, k):
+            di, dj = OFFSETS[k]
+            top = -di
             chunks = slice(pair * PAIR, (pair + 1) * PAIR)
-            for k in range(K):
-                di, dj = OFFSETS[k]
-                top = -di
-                products = terms[:, k, :, top * GRID : T].rearrange("p c (i j) -> p c i j", j=GRID)
-                if k == 0:
-                    nc.scalar.activation(
-                        out=products, in_=padded_rows(b, chunks, 0), func=ACT.Square
-                    )
-                else:
-                    nc.vector.tensor_tensor(
-                        out=products,
-                        in0=padded_rows(b, chunks, 0)[:, :, top:GRID, :],
-                        in1=padded_rows(b, chunks, dj)[:, :, 0 : GRID - top, :],
-                        op=ALU.mult,
-                    )
+            products = products_of(b, pair, k)
+            here = padded_rows(b, chunks, 0)[:, :, top:GRID, :]
+            there = padded_rows(b, chunks, dj)[:, :, 0 : GRID - top, :]
+            if k == OWN:
+                nc.scalar.activation(out=products, in_=here, func=ACT.Square)
+            elif k < on_vector_count(b):
                 for c in range(PAIR):
+                    ch = pair * PAIR + c
+                    nc.vector.scalar_tensor_tensor(
+                        out=products[:, c],
+                        in0=here[:, c],
+                        scalar=coef[b][:, k, ch : ch + 1],
+                        in1=there[:, c],
+                        op0=ALU.mult,
+                        op1=ALU.mult,
+                    )
+            else:
+                nc.gpsimd.tensor_tensor(out=products, in0=here, in1=there, op=ALU.mult)
+
+        def clamp(b, pair, k):
+            top = -OFFSETS[k][0]
+            terms = terms_of(b, pair)
+            if k < on_vector_count(b):
+                term = terms[:, k, :, top * GRID : T]
+                nc.scalar.activation(out=term, in_=term, func=ACT.Relu, bias=minus_eps[:])
+            else:
+                for c in range(PAIR):
+                    ch = pair * PAIR + c
+                    term = terms[:, k, c, top * GRID : T]
                     nc.scalar.activation(
-                        out=terms[:, k, c, top * GRID : T],
-                        in_=terms[:, k, c, top * GRID : T],
+                        out=term,
+                        in_=term,
                         func=ACT.Relu,
-                        scale=coef[b][:, k, pair * PAIR + c : pair * PAIR + c + 1],
+                        scale=coef[b][:, k, ch : ch + 1],
                         bias=minus_eps[:],
                     )
 
+        def vector_clamps(b):
+            if b == B - 1:
+                return V_CLAMPS_LAST
+            return V_CLAMPS
+
+        def clamp_on_vector(b, pair):
+            term = terms_of(b, pair)[:, 0 : vector_clamps(b), :, 0:T]
+            nc.vector.tensor_scalar(term, term, -EPS_GEM_CUBED, 0.0, op0=ALU.add, op1=ALU.max)
+
         def window_sum(b, pair):
-            terms = term_tiles[(b * (CH // PAIR) + pair) % 3]
+            terms = terms_of(b, pair)
             if pair == 0:
                 for h in range(H):
                     acc[b, h] = acc_psum.tile([P, C], F32, name="acc")
@@ -245,169 +323,319 @@ def tile_tokenmudule_pa_s_kernel(tc, patch_tokens, fc1_w, fc1_b, out):
                             stop=(i == len(TERMS) - 1),
                         )
 
-        def square_sum(on_vector, values, unread, total):
-            if on_vector:
-                nc.vector.scalar_tensor_tensor(
-                    out=unread,
-                    in0=values,
-                    scalar=1.0,
-                    in1=values,
-                    op0=ALU.mult,
-                    op1=ALU.mult,
-                    accum_out=total,
-                )
-            else:
-                nc.scalar.activation(out=unread, in_=values, func=ACT.Square, accum_out=total)
+        def halves(b):
+            return [slice(0, 1), slice(1, 2)] if b == B - 1 else [slice(0, 2)]
 
-        def scale_rows(on_vector, scaled, values, factor):
-            if on_vector:
-                nc.vector.tensor_scalar_mul(scaled, values, factor)
-            else:
-                nc.scalar.activation(out=scaled, in_=values, func=ACT.Copy, scale=factor)
+        def pooled_of(images):
+            log_sum(images)
+            exp_sum(images)
 
-        def copy_from_psum(on_vector, copied, values):
-            if on_vector:
-                nc.vector.tensor_copy(out=copied, in_=values)
-            else:
-                nc.scalar.copy(out=copied, in_=values)
-
-        def close_round(first, on_vector):
-            step = steps_done.get(first, 0)
-            steps_done[first] = step + 1
-            images = range(first, first + ROUND)
-            if step == 0:
-                for b in images:
-                    pooled[b] = pooled_pool.tile([P, H, C], F32, name="pooled")
-                    for h in range(H):
-                        nc.scalar.activation(
-                            out=pooled[b][:, h, :],
-                            in_=acc[b, h][:],
-                            func=ACT.Ln,
-                            scale=1.0 / len(TERMS),
-                            bias=plus_eps[:],
-                        )
-            elif step == 1:
-                for b in images:
+        def log_sum(images):
+            for b in images:
+                pooled[b] = pooled_pool.tile([P, H, C], F32, name="pooled")
+                for h in range(H):
                     nc.scalar.activation(
-                        out=pooled[b][:], in_=pooled[b][:], func=ACT.Exp, scale=1.0 / 3.0
+                        out=pooled[b][:, h, :],
+                        in_=acc[b, h][:],
+                        func=ACT.Ln,
+                        scale=1.0 / len(TERMS),
+                        bias=plus_eps[:],
                     )
-            elif step == 2:
-                for b in images:
-                    nc.vector.tensor_tensor(
-                        out=pooled[b][:], in0=pooled[b][:], in1=x_nat[:, b], op=ALU.add
+
+        def exp_sum(images):
+            for b in images:
+                for h in halves(b):
+                    nc.scalar.activation(
+                        out=pooled[b][:, h], in_=pooled[b][:, h], func=ACT.Exp, scale=1.0 / 3.0
                     )
-            elif step == 3:
-                r_sq = tail_pool.tile([P, ROUND, H], F32, name="r_sq")
-                closing[first, "r_sq"] = r_sq
-                for b in images:
-                    unread = tail_pool.tile([P, H, C], F32, name="unread_r")
-                    for h in range(H):
-                        square_sum(
-                            on_vector,
-                            pooled[b][:, h, :],
-                            unread[:, h, :],
-                            r_sq[:, b - first, h : h + 1],
-                        )
-            elif step == 4:
-                floored = tail_pool.tile([P, ROUND, H], F32, name="r_floored")
-                nc.vector.tensor_scalar_max(floored[:], closing[first, "r_sq"][:], EPS_NORM_SQUARED)
-                r_norm = tail_pool.tile([P, ROUND, H], F32, name="r_norm")
-                closing[first, "r_norm"] = r_norm
+
+        def add_x_tasks(images):
+            return [
+                lambda b=b, h=h: nc.vector.tensor_tensor(
+                    out=pooled[b][:, h], in0=pooled[b][:, h], in1=x_nat[:, b, h], op=ALU.add
+                )
+                for b in images
+                for h in halves(b)
+            ]
+
+        def square_sums(images):
+            for b in images:
+                r_sq = tail_pool.tile([P, H], F32, name="r_sq")
+                closing[b, "r_sq"] = r_sq
+                for h in range(H):
+                    unread = unread_pool.tile([P, C], BF16, name="unread_r")
+                    nc.scalar.activation(
+                        out=unread[:],
+                        in_=pooled[b][:, h, :],
+                        func=ACT.Square,
+                        accum_out=r_sq[:, h : h + 1],
+                    )
+
+        def square_sums_on_vector(images):
+            for b in images:
+                r_sq = tail_pool.tile([P, H], F32, name="r_sq")
+                closing[b, "r_sq"] = r_sq
+                for h in range(H):
+                    unread = unread_pool.tile([P, C], BF16, name="unread_r")
+                    nc.vector.scalar_tensor_tensor(
+                        out=unread[:],
+                        in0=pooled[b][:, h, :],
+                        scalar=1.0,
+                        in1=pooled[b][:, h, :],
+                        op0=ALU.mult,
+                        op1=ALU.mult,
+                        accum_out=r_sq[:, h : h + 1],
+                    )
+
+        def square_sums_split(b):
+            r_sq = tail_pool.tile([P, H], F32, name="r_sq")
+            closing[b, "r_sq"] = r_sq
+            unread = unread_pool.tile([P, C], BF16, name="unread_r")
+            nc.vector.scalar_tensor_tensor(
+                out=unread[:],
+                in0=pooled[b][:, 0, :],
+                scalar=1.0,
+                in1=pooled[b][:, 0, :],
+                op0=ALU.mult,
+                op1=ALU.mult,
+                accum_out=r_sq[:, 0:1],
+            )
+            unread = unread_pool.tile([P, C], BF16, name="unread_r")
+            nc.scalar.activation(
+                out=unread[:], in_=pooled[b][:, 1, :], func=ACT.Square, accum_out=r_sq[:, 1:2]
+            )
+
+        def roots(images):
+            for b in images:
+                floored = tail_pool.tile([P, H], F32, name="r_floored")
+                nc.vector.tensor_scalar_max(floored[:], closing[b, "r_sq"][:], EPS_NORM_SQUARED)
+                r_norm = tail_pool.tile([P, H], F32, name="r_norm")
+                closing[b, "r_norm"] = r_norm
                 nc.scalar.activation(out=r_norm[:], in_=floored[:], func=ACT.Sqrt)
-            elif step == 5:
-                inv_r = tail_pool.tile([P, ROUND, H], F32, name="inv_r")
-                nc.vector.reciprocal(inv_r[:], closing[first, "r_norm"][:])
-                for b in images:
-                    tokens = tail_pool.tile([P, H, C], BF16, name="tokens")
-                    closing[b, "tokens"] = tokens
-                    for h in range(H):
-                        scale_rows(
-                            on_vector,
-                            tokens[:, h, :],
+
+        def scale_tokens_tasks(images):
+            tasks = []
+            for b in images:
+                inv_r = tail_pool.tile([P, H], F32, name="inv_r")
+                closing[b, "inv_r"] = inv_r
+                tokens = tail_pool.tile([P, H, C], BF16, name="tokens")
+                closing[b, "tokens"] = tokens
+                tasks.append(
+                    lambda b=b: nc.vector.reciprocal(closing[b, "inv_r"][:], closing[b, "r_norm"][:])
+                )
+            for b in images:
+                for h in range(H):
+                    tasks.append(
+                        lambda b=b, h=h: nc.vector.tensor_scalar_mul(
+                            closing[b, "tokens"][:, h, :],
                             pooled[b][:, h, :],
-                            inv_r[:, b - first, h : h + 1],
+                            closing[b, "inv_r"][:, h : h + 1],
                         )
-                for b in images:
-                    tokens = closing[b, "tokens"]
-                    words = tokens[:].rearrange("p h c -> p (h c)").bitcast(F32)
+                    )
+            return tasks
+
+        def turn_tokens(images):
+            for b in images:
+                words = closing[b, "tokens"][:].rearrange("p h c -> p (h c)").bitcast(F32)
+                if b < B - 4:
                     tokT = proj_psum.tile([P, H, 2, P], F32, name="proj")
-                    for h in range(H):
-                        for u in range(2):
-                            nc.tensor.transpose(
-                                tokT[:, h, u, :],
-                                words[:, h * (C // 2) + u : (h + 1) * (C // 2) : 2],
-                                ident_f[:],
-                            )
-                    grouped = tail_pool.tile([P, H * P * PACK], BF16, name="grouped", align_bytes=64)
-                    closing[b, "grouped"] = grouped
-                    copy_from_psum(
-                        on_vector,
-                        grouped[:].bitcast(F32).rearrange("p (h r u) -> p h r u", h=H, u=2),
-                        tokT[:].rearrange("p h u r -> p h r u"),
-                    )
-            elif step == 6:
-                for b in images:
-                    codes = tail_pool.tile([P, H * P], U32, name="codes", align_bytes=64)
-                    scales = tail_pool.tile([P, H * P], U8, name="scales", align_bytes=64)
-                    nc.vector.quantize_mx(
-                        out=codes[:].bitcast(FP8X4),
-                        scales=scales[:],
-                        in_=closing[b, "grouped"][:],
-                    )
-                    product = proj_psum.tile([P, H, F], F32, name="proj")
-                    closing[b, "product"] = product
-                    for h in range(H):
-                        nc.tensor.matmul_mx(
-                            out=product[:, h, :],
-                            lhsT=codes[:, h * P : (h + 1) * P].bitcast(FP8X4),
-                            lhsT_scale=scales[:, h * P : (h + 1) * P],
-                            rhs=w_codes[:].bitcast(FP8X4),
-                            rhs_scale=w_scales[:],
-                            start=True,
-                            stop=True,
+                else:
+                    tokT = qT_psum.tile([P, H, 2, P], F32, name="qT")
+                for h in range(H):
+                    for u in range(2):
+                        nc.tensor.transpose(
+                            tokT[:, h, u, :],
+                            words[:, h * (C // 2) + u : (h + 1) * (C // 2) : 2],
+                            ident_f[:],
                         )
-            else:
-                for b in images:
-                    nc.vector.tensor_tensor(
-                        out=pre_act[:, b],
-                        in0=closing[b, "product"][:],
-                        in1=bias[:].unsqueeze(1).to_broadcast([P, H, F]),
-                        op=ALU.add,
+                grouped = tail_pool.tile([P, H * P * PACK], BF16, name="grouped", align_bytes=64)
+                closing[b, "grouped"] = grouped
+                nc.scalar.copy(
+                    out=grouped[:].bitcast(F32).rearrange("p (h r u) -> p h r u", h=H, u=2),
+                    in_=tokT[:].rearrange("p h u r -> p h r u"),
+                )
+
+        def project(images):
+            for b in images:
+                codes = tail_pool.tile([P, H * P], U32, name="codes", align_bytes=64)
+                scales = tail_pool.tile([P, H * P], U8, name="scales", align_bytes=64)
+                nc.vector.quantize_mx(
+                    out=codes[:].bitcast(FP8X4), scales=scales[:], in_=closing[b, "grouped"][:]
+                )
+                product = proj_psum.tile([P, H, F], F32, name="proj")
+                for h in range(H):
+                    nc.tensor.matmul_mx(
+                        out=product[:, h, :],
+                        lhsT=codes[:, h * P : (h + 1) * P].bitcast(FP8X4),
+                        lhsT_scale=scales[:, h * P : (h + 1) * P],
+                        rhs=w_codes[:].bitcast(FP8X4),
+                        rhs_scale=w_scales[:],
+                        start=True,
+                        stop=True,
                     )
+                nc.vector.tensor_tensor(
+                    out=pre_act[:, b],
+                    in0=product[:],
+                    in1=bias[:].unsqueeze(1).to_broadcast([P, H, F]),
+                    op=ALU.add,
+                )
 
-        for b in range(2):
-            for i in range(B // 2):
-                square_x(b * (B // 2) + i)
-            for k in range(1, K):
-                sum_products(b, k)
-            start_coefficients(b)
+        def gpsimd_products(b, pair):
+            for k in range(on_vector_count(b), OWN):
+                multiply(b, pair, k)
+
+        def round_ending(b):
+            for images in ROUNDS:
+                if images[-1] == b:
+                    return images
+            return ()
+
+        def norms(b, half, extra):
+            for k in range(OWN):
+                sum_products(b, k, half)
+                for step in extra[k : k + 1]:
+                    step()
+
+        square_x(0, 2)
+        transpose_q(0, 0)
+        copy_q(0, 0)
+        transpose_q(0, 1)
+        copy_q(0, 1, on_vector=True)
+        square_x(1)
         transpose_x(0)
-        finish_coefficients(0)
-        scale_cubes(0)
+        for half in range(2):
+            norms(0, half, [])
+            sum_squares(0, half)
+            transpose_q(1, half)
+            if half == 0:
+                copy_q(1, half)
+        start_coefficients(0)
 
-        for b in range(B):
-            if b + 1 < B:
-                transpose_x(b + 1)
-            for pair in range(CH // PAIR):
-                window_terms(b, pair)
-                window_sum(b, pair)
-            if b + 1 < B:
-                finish_coefficients(b + 1)
-                scale_cubes(b + 1)
+        for b in range(-1, B - 2):
+            quantised = round_ending(b - 3)
+            steps = coefficient_steps(b + 1) if b + 1 < B else []
+            if b >= 0:
+                if b + 1 < B:
+                    transpose_x(b + 1)
+                for pair in range(CH // PAIR):
+                    for k in range(on_vector_count(b)):
+                        multiply(b, pair, k)
+                    multiply(b, pair, OWN)
+                    for k in range(on_vector_count(b), K):
+                        clamp(b, pair, k)
+                    if pair == 0:
+                        project(quantised)
+                    clamp_on_vector(b, pair)
+                    for k in range(vector_clamps(b), on_vector_count(b)):
+                        clamp(b, pair, k)
+                    window_sum(b, pair)
             if b + 2 < B:
-                for k in range(1, K):
-                    sum_products(b + 2, k)
-                    if k % 2 == 0:
-                        for first in range(0, b, ROUND):
-                            if steps_done.get(first, 0) < CLOSING_STEPS:
-                                close_round(first, False)
+                copy_q(b + 2, 1)
+                for half in range(2):
+                    sum_squares(b + 2, half)
+            if b + 3 < B:
+                square_x(b + 3)
+            tasks = add_x_tasks(round_ending(b - 1)) + scale_tokens_tasks(round_ending(b - 2))
+            while tasks or steps:
+                for task in steps[0:1] + tasks[0:1]:
+                    task()
+                steps = steps[1:]
+                tasks = tasks[1:]
+            if b + 1 < B:
+                for pair in range(CH // PAIR):
+                    scale_cubes(b + 1, pair)
+                    gpsimd_products(b + 1, pair)
+            if b + 2 < B:
+                norms(b + 2, 0, [])
+                if b + 3 < B:
+                    transpose_q(b + 3, 0)
+            square_sums(round_ending(b - 1))
+            if b + 3 < B:
+                copy_q(b + 3, 0)
+            turn_tokens(round_ending(b - 2))
+            if b + 2 < B:
+                norms(b + 2, 1, [])
+                if b + 3 < B:
+                    transpose_q(b + 3, 1)
+            pooled_of(round_ending(b))
+            if b + 2 < B:
                 start_coefficients(b + 2)
-        for first in range(0, B, ROUND):
-            while steps_done.get(first, 0) < CLOSING_STEPS:
-                close_round(first, True)
+            roots(round_ending(b - 1))
+        def preload(func):
+            nc.scalar.activation(out=scratch[:], in_=scratch[:], func=func)
+
+        def vector_products(b, pair, ks):
+            for k in ks:
+                multiply(b, pair, k)
+
+        b = B - 2
+        transpose_x(b + 1)
+        for pair in range(CH // PAIR):
+            for k in range(on_vector_count(b)):
+                multiply(b, pair, k)
+            multiply(b, pair, OWN)
+            for k in range(on_vector_count(b), K):
+                clamp(b, pair, k)
+            if pair == 0:
+                project(round_ending(b - 3))
+            clamp_on_vector(b, pair)
+            for k in range(vector_clamps(b), on_vector_count(b)):
+                clamp(b, pair, k)
+            window_sum(b, pair)
+        tasks = add_x_tasks(round_ending(b - 1))
+        steps = coefficient_steps(b + 1)
+        while tasks or steps:
+            for task in steps[0:1] + tasks[0:1]:
+                task()
+            steps = steps[1:]
+            tasks = tasks[1:]
+        square_sums(round_ending(b - 1))
+        b = B - 1
+        for pair in range(CH // PAIR):
+            scale_cubes(b, pair)
+            vector_products(b, pair, range(0, vector_clamps(b)))
+            multiply(b, pair, OWN)
+            tasks = scale_tokens_tasks(round_ending(b - 2)) if pair == 1 else []
+            for task in tasks:
+                task()
+            vector_products(b, pair, range(vector_clamps(b), OWN))
+            if pair == 1:
+                log_sum(round_ending(b - 1))
+            clamp(b, pair, OWN)
+            clamp_on_vector(b, pair)
+            for k in range(vector_clamps(b), OWN):
+                clamp(b, pair, k)
+            if pair == 0:
+                roots(round_ending(b - 2))
+            else:
+                turn_tokens(round_ending(b - 2))
+            window_sum(b, pair)
+        exp_sum(round_ending(b - 1))
+        for task in add_x_tasks(round_ending(b - 1)):
+            task()
+        square_sums_on_vector(round_ending(b - 1))
+        project(round_ending(b - 2))
+        log_sum(round_ending(b))
+        exp_sum(round_ending(b))
+        preload(ACT.Sqrt)
+        roots(round_ending(b - 1))
+        tasks = add_x_tasks(round_ending(b))
+        tasks[0]()
+        for task in scale_tokens_tasks(round_ending(b - 1)):
+            task()
+        tasks[1]()
+        turn_tokens(round_ending(b - 1))
+        square_sums_split(b)
+        roots(round_ending(b))
+        preload(ACT.Gelu)
+        project(round_ending(b - 1))
+        for task in scale_tokens_tasks(round_ending(b)):
+            task()
+        turn_tokens(round_ending(b))
+        project(round_ending(b))
 
         stored = out.rearrange("b (h p) f -> p b h f", p=P)
-        for first in range(0, B, ROUND):
-            images = slice(first, first + ROUND)
+        for first in range(0, B, 2):
+            images = slice(first, first + 2)
             nc.scalar.activation(out=result[:, images], in_=pre_act[:, images], func=ACT.Gelu)
             nc.sync.dma_start(out=stored[:, images], in_=result[:, images])

@@ -5,6 +5,7 @@ from concourse.masks import make_identity
 
 F32 = mybir.dt.float32
 BF16 = mybir.dt.bfloat16
+I32 = mybir.dt.int32
 U32 = mybir.dt.uint32
 U8 = mybir.dt.uint8
 FP8X4 = mybir.dt.float8_e4m3fn_x4
@@ -29,6 +30,8 @@ OWN = OFFSETS.index((0, 0))
 ON_V = 3
 V_CLAMPS = 3
 V_CLAMPS_LAST = 4
+V_CLAMPS_EVEN = 1
+SMALL_FROM = 3
 K_LEFT = OFFSETS.index((0, -1))
 TERMS = [(k, 0) for k in range(K)] + [(K_LEFT, 1)]
 
@@ -40,6 +43,7 @@ TERM_COLS = T + 8
 
 EPS_GEM_CUBED = 1e-18
 EPS_NORM_SQUARED = 1e-24
+RSQRT_BITS = 0x5F3759DF
 
 TERM_TILES = 5
 PAIR = 2
@@ -102,15 +106,10 @@ def tile_tokenmudule_pa_s_kernel(tc, patch_tokens, fc1_w, fc1_b, out):
         w_grouped = keep.tile([P, F, PACK], BF16, align_bytes=64)
         w_codes = keep.tile([P, F], U32, align_bytes=64)
         w_scales = keep.tile([P, F], U8, align_bytes=64)
-        nc.vector.tensor_copy(out=w_grouped[:], in_=w_raw[:].rearrange("p t f -> p f t"))
-        nc.vector.quantize_mx(
-            out=w_codes[:].bitcast(FP8X4),
-            scales=w_scales[:],
-            in_=w_grouped[:].rearrange("p f t -> p (f t)"),
-        )
 
-        scratch = keep.tile([P, 1], F32)
-        nc.vector.memset(scratch[:], 1.0)
+        one = keep.tile([P, 1], F32)
+        nc.vector.memset(one[:], 1.0)
+        unused = keep.tile([P, 1], F32)
         own_sq = keep.tile([P, B, CH], F32)
         pre_act = keep.tile([P, B, H, F], F32)
         result = keep.tile([P, B, H, F], F32)
@@ -299,7 +298,7 @@ def tile_tokenmudule_pa_s_kernel(tc, patch_tokens, fc1_w, fc1_b, out):
         def vector_clamps(b):
             if b == B - 1:
                 return V_CLAMPS_LAST
-            return V_CLAMPS
+            return V_CLAMPS if b % 2 == 1 or b == B - 2 else V_CLAMPS_EVEN
 
         def clamp_on_vector(b, pair):
             term = terms_of(b, pair)[:, 0 : vector_clamps(b), :, 0:T]
@@ -309,7 +308,10 @@ def tile_tokenmudule_pa_s_kernel(tc, patch_tokens, fc1_w, fc1_b, out):
             terms = terms_of(b, pair)
             if pair == 0:
                 for h in range(H):
-                    acc[b, h] = acc_psum.tile([P, C], F32, name="acc")
+                    if b == B - 2:
+                        acc[b, h] = qT_psum.tile([P, C], F32, name="qT")
+                    else:
+                        acc[b, h] = acc_psum.tile([P, C], F32, name="acc")
             for c in range(PAIR):
                 ch = pair * PAIR + c
                 for i, (k, ahead) in enumerate(TERMS):
@@ -324,7 +326,7 @@ def tile_tokenmudule_pa_s_kernel(tc, patch_tokens, fc1_w, fc1_b, out):
                         )
 
         def halves(b):
-            return [slice(0, 1), slice(1, 2)] if b == B - 1 else [slice(0, 2)]
+            return [slice(0, 1), slice(1, 2)] if b >= B - 2 else [slice(0, 2)]
 
         def pooled_of(images):
             log_sum(images)
@@ -413,16 +415,67 @@ def tile_tokenmudule_pa_s_kernel(tc, patch_tokens, fc1_w, fc1_b, out):
                 closing[b, "r_norm"] = r_norm
                 nc.scalar.activation(out=r_norm[:], in_=floored[:], func=ACT.Sqrt)
 
-        def scale_tokens_tasks(images):
+        def newton_roots(images):
+            for b in images:
+                m = tail_pool.tile([P, H], F32, name="rm")
+                seed = tail_pool.tile([P, H], I32, name="rseed")
+                t = tail_pool.tile([P, H], F32, name="rt")
+                u = tail_pool.tile([P, H], F32, name="ru")
+                y = tail_pool.tile([P, H], F32, name="inv_r")
+                closing[b, "inv_r"] = y
+                closing[b, "newton"] = (m, seed, t, u, y)
+
+            def on_all(step):
+                for b in images:
+                    step(*closing[b, "newton"], closing[b, "r_sq"])
+
+            V = nc.vector
+            on_all(lambda m, seed, t, u, y, r: V.tensor_scalar_max(m[:], r[:], EPS_NORM_SQUARED))
+            on_all(
+                lambda m, seed, t, u, y, r: V.tensor_single_scalar(
+                    seed[:], m[:].bitcast(I32), 1, ALU.logical_shift_right
+                )
+            )
+            on_all(
+                lambda m, seed, t, u, y, r: V.tensor_scalar(
+                    seed[:], seed[:], -1.0, float(RSQRT_BITS), op0=ALU.mult, op1=ALU.add
+                )
+            )
+            for i in range(3):
+
+                def last(seed, y, i=i):
+                    return seed[:].bitcast(F32) if i == 0 else y[:]
+
+                on_all(
+                    lambda m, seed, t, u, y, r: V.scalar_tensor_tensor(
+                        out=t[:], in0=last(seed, y), scalar=1.0, in1=m[:], op0=ALU.mult, op1=ALU.mult
+                    )
+                )
+                on_all(
+                    lambda m, seed, t, u, y, r: V.scalar_tensor_tensor(
+                        out=u[:], in0=t[:], scalar=-0.5, in1=last(seed, y), op0=ALU.mult, op1=ALU.mult
+                    )
+                )
+                on_all(
+                    lambda m, seed, t, u, y, r: V.scalar_tensor_tensor(
+                        out=y[:], in0=u[:], scalar=1.5, in1=last(seed, y), op0=ALU.add, op1=ALU.mult
+                    )
+                )
+
+        def scale_tokens_tasks(images, inverse=True):
             tasks = []
             for b in images:
-                inv_r = tail_pool.tile([P, H], F32, name="inv_r")
-                closing[b, "inv_r"] = inv_r
+                if inverse:
+                    inv_r = tail_pool.tile([P, H], F32, name="inv_r")
+                    closing[b, "inv_r"] = inv_r
                 tokens = tail_pool.tile([P, H, C], BF16, name="tokens")
                 closing[b, "tokens"] = tokens
-                tasks.append(
-                    lambda b=b: nc.vector.reciprocal(closing[b, "inv_r"][:], closing[b, "r_norm"][:])
-                )
+                if inverse:
+                    tasks.append(
+                        lambda b=b: nc.vector.reciprocal(
+                            closing[b, "inv_r"][:], closing[b, "r_norm"][:]
+                        )
+                    )
             for b in images:
                 for h in range(H):
                     tasks.append(
@@ -437,10 +490,10 @@ def tile_tokenmudule_pa_s_kernel(tc, patch_tokens, fc1_w, fc1_b, out):
         def turn_tokens(images):
             for b in images:
                 words = closing[b, "tokens"][:].rearrange("p h c -> p (h c)").bitcast(F32)
-                if b < B - 4:
+                if b < B - 4 or b % 2 == 0:
                     tokT = proj_psum.tile([P, H, 2, P], F32, name="proj")
                 else:
-                    tokT = qT_psum.tile([P, H, 2, P], F32, name="qT")
+                    tokT = xT_psum.tile([P, H, 2, P], F32, name="xT")
                 for h in range(H):
                     for u in range(2):
                         nc.tensor.transpose(
@@ -457,12 +510,21 @@ def tile_tokenmudule_pa_s_kernel(tc, patch_tokens, fc1_w, fc1_b, out):
 
         def project(images):
             for b in images:
+                project_one(b)
+                add_bias(b)
+
+        def project_one(b):
+            if True:
                 codes = tail_pool.tile([P, H * P], U32, name="codes", align_bytes=64)
                 scales = tail_pool.tile([P, H * P], U8, name="scales", align_bytes=64)
                 nc.vector.quantize_mx(
                     out=codes[:].bitcast(FP8X4), scales=scales[:], in_=closing[b, "grouped"][:]
                 )
-                product = proj_psum.tile([P, H, F], F32, name="proj")
+                if b < B - 4 or b % 2 == 0:
+                    product = proj_psum.tile([P, H, F], F32, name="proj")
+                else:
+                    product = xT_psum.tile([P, H, F], F32, name="xT")
+                closing[b, "product"] = product
                 for h in range(H):
                     nc.tensor.matmul_mx(
                         out=product[:, h, :],
@@ -473,9 +535,12 @@ def tile_tokenmudule_pa_s_kernel(tc, patch_tokens, fc1_w, fc1_b, out):
                         start=True,
                         stop=True,
                     )
+
+        def add_bias(b):
+            if True:
                 nc.vector.tensor_tensor(
                     out=pre_act[:, b],
-                    in0=product[:],
+                    in0=closing[b, "product"][:],
                     in1=bias[:].unsqueeze(1).to_broadcast([P, H, F]),
                     op=ALU.add,
                 )
@@ -496,7 +561,45 @@ def tile_tokenmudule_pa_s_kernel(tc, patch_tokens, fc1_w, fc1_b, out):
                 for step in extra[k : k + 1]:
                     step()
 
-        square_x(0, 2)
+        def preload(func):
+            nc.scalar.activation(out=unused[:], in_=one[:], func=func)
+
+        def run(main, between):
+            for step in main:
+                step()
+                for small in between[0:1]:
+                    small()
+                between = between[1:]
+            for small in between:
+                small()
+
+        def product_steps(b, pair):
+            return [lambda k=k: multiply(b, pair, k) for k in range(on_vector_count(b))]
+
+        def vector_phase(b, small, tasks, quantised):
+            first, second = product_steps(b, 0), product_steps(b, 1)
+            closing_steps = []
+            for image in quantised:
+                closing_steps.append(lambda image=image: project_one(image))
+                closing_steps.append(lambda image=image: add_bias(image))
+            main = []
+            for step in first + second[0:1]:
+                main += closing_steps[0:1] + [step]
+                closing_steps = closing_steps[1:]
+            main.append(lambda: clamp_on_vector(b, 0))
+            main += second[1:] + tasks[0:1]
+            main.append(lambda: clamp_on_vector(b, 1))
+            main += tasks[1:]
+            run(main, [lambda: None] * SMALL_FROM + small)
+            for pair in range(CH // PAIR):
+                multiply(b, pair, OWN)
+                for k in list(range(on_vector_count(b), K)) + list(
+                    range(vector_clamps(b), on_vector_count(b))
+                ):
+                    clamp(b, pair, k)
+                window_sum(b, pair)
+
+        square_x(0, 4)
         transpose_q(0, 0)
         copy_q(0, 0)
         transpose_q(0, 1)
@@ -509,38 +612,27 @@ def tile_tokenmudule_pa_s_kernel(tc, patch_tokens, fc1_w, fc1_b, out):
             transpose_q(1, half)
             if half == 0:
                 copy_q(1, half)
+        nc.vector.tensor_copy(out=w_grouped[:], in_=w_raw[:].rearrange("p t f -> p f t"))
+        nc.vector.quantize_mx(
+            out=w_codes[:].bitcast(FP8X4),
+            scales=w_scales[:],
+            in_=w_grouped[:].rearrange("p f t -> p (f t)"),
+        )
         start_coefficients(0)
 
         for b in range(-1, B - 2):
-            quantised = round_ending(b - 3)
-            steps = coefficient_steps(b + 1) if b + 1 < B else []
+            small = coefficient_steps(b + 1)
+            tasks = add_x_tasks(round_ending(b - 1)) + scale_tokens_tasks(round_ending(b - 2))
             if b >= 0:
-                if b + 1 < B:
-                    transpose_x(b + 1)
-                for pair in range(CH // PAIR):
-                    for k in range(on_vector_count(b)):
-                        multiply(b, pair, k)
-                    multiply(b, pair, OWN)
-                    for k in range(on_vector_count(b), K):
-                        clamp(b, pair, k)
-                    if pair == 0:
-                        project(quantised)
-                    clamp_on_vector(b, pair)
-                    for k in range(vector_clamps(b), on_vector_count(b)):
-                        clamp(b, pair, k)
-                    window_sum(b, pair)
-            if b + 2 < B:
-                copy_q(b + 2, 1)
-                for half in range(2):
-                    sum_squares(b + 2, half)
+                transpose_x(b + 1)
+                vector_phase(b, small, tasks, round_ending(b - 3))
+            copy_q(b + 2, 1)
+            for half in range(2):
+                sum_squares(b + 2, half)
             if b + 3 < B:
                 square_x(b + 3)
-            tasks = add_x_tasks(round_ending(b - 1)) + scale_tokens_tasks(round_ending(b - 2))
-            while tasks or steps:
-                for task in steps[0:1] + tasks[0:1]:
-                    task()
-                steps = steps[1:]
-                tasks = tasks[1:]
+            if b < 0:
+                run([], small)
             if b + 1 < B:
                 for pair in range(CH // PAIR):
                     scale_cubes(b + 1, pair)
@@ -550,89 +642,64 @@ def tile_tokenmudule_pa_s_kernel(tc, patch_tokens, fc1_w, fc1_b, out):
                 if b + 3 < B:
                     transpose_q(b + 3, 0)
             square_sums(round_ending(b - 1))
+            summed = round_ending(b) if b < B - 3 else ()
+            if summed:
+                preload(ACT.Ln)
+            log_sum(summed)
             if b + 3 < B:
                 copy_q(b + 3, 0)
+            exp_sum(summed)
             turn_tokens(round_ending(b - 2))
             if b + 2 < B:
                 norms(b + 2, 1, [])
                 if b + 3 < B:
                     transpose_q(b + 3, 1)
-            pooled_of(round_ending(b))
             if b + 2 < B:
                 start_coefficients(b + 2)
             roots(round_ending(b - 1))
-        def preload(func):
-            nc.scalar.activation(out=scratch[:], in_=scratch[:], func=func)
-
         def vector_products(b, pair, ks):
             for k in ks:
                 multiply(b, pair, k)
 
         b = B - 2
         transpose_x(b + 1)
-        for pair in range(CH // PAIR):
-            for k in range(on_vector_count(b)):
-                multiply(b, pair, k)
-            multiply(b, pair, OWN)
-            for k in range(on_vector_count(b), K):
-                clamp(b, pair, k)
-            if pair == 0:
-                project(round_ending(b - 3))
-            clamp_on_vector(b, pair)
-            for k in range(vector_clamps(b), on_vector_count(b)):
-                clamp(b, pair, k)
-            window_sum(b, pair)
-        tasks = add_x_tasks(round_ending(b - 1))
-        steps = coefficient_steps(b + 1)
-        while tasks or steps:
-            for task in steps[0:1] + tasks[0:1]:
-                task()
-            steps = steps[1:]
-            tasks = tasks[1:]
-        square_sums(round_ending(b - 1))
+        vector_phase(b, coefficient_steps(b + 1), [], round_ending(b - 3))
+        pooled_of(round_ending(b - 1))
         b = B - 1
         for pair in range(CH // PAIR):
             scale_cubes(b, pair)
-            vector_products(b, pair, range(0, vector_clamps(b)))
+            steps = product_steps(b, pair)
+            run(steps[0 : vector_clamps(b)], [])
             multiply(b, pair, OWN)
-            tasks = scale_tokens_tasks(round_ending(b - 2)) if pair == 1 else []
-            for task in tasks:
-                task()
-            vector_products(b, pair, range(vector_clamps(b), OWN))
-            if pair == 1:
-                log_sum(round_ending(b - 1))
             clamp(b, pair, OWN)
+            run(steps[vector_clamps(b) :], [])
             clamp_on_vector(b, pair)
             for k in range(vector_clamps(b), OWN):
                 clamp(b, pair, k)
-            if pair == 0:
-                roots(round_ending(b - 2))
-            else:
-                turn_tokens(round_ending(b - 2))
             window_sum(b, pair)
-        exp_sum(round_ending(b - 1))
-        for task in add_x_tasks(round_ending(b - 1)):
+        for task in add_x_tasks(round_ending(b - 2)):
             task()
-        square_sums_on_vector(round_ending(b - 1))
-        project(round_ending(b - 2))
-        log_sum(round_ending(b))
-        exp_sum(round_ending(b))
+        square_sums_on_vector(round_ending(b - 2))
+        newton_roots(round_ending(b - 2))
+        for task in scale_tokens_tasks(round_ending(b - 2), inverse=False):
+            task()
+        log_sum((b - 1, b))
+        exp_sum((b, b - 1))
         preload(ACT.Sqrt)
-        roots(round_ending(b - 1))
-        tasks = add_x_tasks(round_ending(b))
-        tasks[0]()
-        for task in scale_tokens_tasks(round_ending(b - 1)):
-            task()
-        tasks[1]()
-        turn_tokens(round_ending(b - 1))
-        square_sums_split(b)
-        roots(round_ending(b))
+        turn_tokens(round_ending(b - 2))
+        for image in (b, b - 1):
+            for task in add_x_tasks((image,)):
+                task()
+            square_sums_split(image)
+        project(round_ending(b - 2))
+        roots((b, b - 1))
         preload(ACT.Gelu)
-        project(round_ending(b - 1))
-        for task in scale_tokens_tasks(round_ending(b)):
-            task()
-        turn_tokens(round_ending(b))
-        project(round_ending(b))
+        for image in (b, b - 1):
+            for task in scale_tokens_tasks((image,)):
+                task()
+            turn_tokens((image,))
+        for image in (b, b - 1):
+            project((image,))
 
         stored = out.rearrange("b (h p) f -> p b h f", p=P)
         for first in range(0, B, 2):

@@ -31,7 +31,8 @@ ON_V = 3
 V_CLAMPS = 3
 V_CLAMPS_LAST = 4
 V_CLAMPS_EVEN = 1
-SMALL_FROM = 3
+SMALL_FROM = 5
+CLOSE_FROM = 2
 K_LEFT = OFFSETS.index((0, -1))
 TERMS = [(k, 0) for k in range(K)] + [(K_LEFT, 1)]
 
@@ -277,6 +278,23 @@ def tile_tokenmudule_pa_s_kernel(tc, patch_tokens, fc1_w, fc1_b, out):
             else:
                 nc.gpsimd.tensor_tensor(out=products, in0=here, in1=there, op=ALU.mult)
 
+        def multiply_chunk(b, ch, k):
+            di, dj = OFFSETS[k]
+            top = -di
+            chunk = slice(ch, ch + 1)
+            nc.vector.scalar_tensor_tensor(
+                out=products_of(b, ch // PAIR, k)[:, ch % PAIR],
+                in0=padded_rows(b, chunk, 0)[:, 0, top:GRID, :],
+                scalar=coef[b][:, k, ch : ch + 1],
+                in1=padded_rows(b, chunk, dj)[:, 0, 0 : GRID - top, :],
+                op0=ALU.mult,
+                op1=ALU.mult,
+            )
+
+        def clamp_chunk(b, ch):
+            term = terms_of(b, ch // PAIR)[:, 0:OWN, ch % PAIR, 0:T]
+            nc.vector.tensor_scalar(term, term, -EPS_GEM_CUBED, 0.0, op0=ALU.add, op1=ALU.max)
+
         def clamp(b, pair, k):
             top = -OFFSETS[k][0]
             terms = terms_of(b, pair)
@@ -305,25 +323,34 @@ def tile_tokenmudule_pa_s_kernel(tc, patch_tokens, fc1_w, fc1_b, out):
             nc.vector.tensor_scalar(term, term, -EPS_GEM_CUBED, 0.0, op0=ALU.add, op1=ALU.max)
 
         def window_sum(b, pair):
-            terms = terms_of(b, pair)
-            if pair == 0:
-                for h in range(H):
+            for c in range(PAIR):
+                window_chunk(b, pair * PAIR + c)
+
+        def window_chunk(b, ch):
+            terms = terms_of(b, ch // PAIR)
+            for h in range(H):
+                if (b, h) not in acc:
                     if b == B - 2:
                         acc[b, h] = qT_psum.tile([P, C], F32, name="qT")
                     else:
                         acc[b, h] = acc_psum.tile([P, C], F32, name="acc")
-            for c in range(PAIR):
-                ch = pair * PAIR + c
-                for i, (k, ahead) in enumerate(TERMS):
-                    for h in range(H):
-                        nc.tensor.matmul(
-                            acc[b, h][:, ch * P : (ch + 1) * P],
-                            lhsT=terms[:, k, c, ahead + h * P : ahead + (h + 1) * P],
-                            rhs=ident_f[:],
-                            is_transpose=True,
-                            start=(i == 0),
-                            stop=(i == len(TERMS) - 1),
-                        )
+            for i, (k, ahead) in enumerate(TERMS):
+                for h in range(H):
+                    nc.tensor.matmul(
+                        acc[b, h][:, ch * P : (ch + 1) * P],
+                        lhsT=terms[:, k, ch % PAIR, ahead + h * P : ahead + (h + 1) * P],
+                        rhs=ident_f[:],
+                        is_transpose=True,
+                        start=(i == 0),
+                        stop=(i == len(TERMS) - 1),
+                    )
+
+        stored = out.rearrange("b (h p) f -> p b h f", p=P)
+
+        def finish(images):
+            these = slice(images[0], images[-1] + 1)
+            nc.scalar.activation(out=result[:, these], in_=pre_act[:, these], func=ACT.Gelu)
+            nc.sync.dma_start(out=stored[:, these], in_=result[:, these])
 
         def halves(b):
             return [slice(0, 1), slice(1, 2)] if b >= B - 2 else [slice(0, 2)]
@@ -487,7 +514,7 @@ def tile_tokenmudule_pa_s_kernel(tc, patch_tokens, fc1_w, fc1_b, out):
                     )
             return tasks
 
-        def turn_tokens(images):
+        def turn_tokens(images, on_vector=False):
             for b in images:
                 words = closing[b, "tokens"][:].rearrange("p h c -> p (h c)").bitcast(F32)
                 if b < B - 4 or b % 2 == 0:
@@ -503,7 +530,8 @@ def tile_tokenmudule_pa_s_kernel(tc, patch_tokens, fc1_w, fc1_b, out):
                         )
                 grouped = tail_pool.tile([P, H * P * PACK], BF16, name="grouped", align_bytes=64)
                 closing[b, "grouped"] = grouped
-                nc.scalar.copy(
+                copy = nc.vector.tensor_copy if on_vector else nc.scalar.copy
+                copy(
                     out=grouped[:].bitcast(F32).rearrange("p (h r u) -> p h r u", h=H, u=2),
                     in_=tokT[:].rearrange("p h u r -> p h r u"),
                 )
@@ -582,14 +610,13 @@ def tile_tokenmudule_pa_s_kernel(tc, patch_tokens, fc1_w, fc1_b, out):
             for image in quantised:
                 closing_steps.append(lambda image=image: project_one(image))
                 closing_steps.append(lambda image=image: add_bias(image))
-            main = []
-            for step in first + second[0:1]:
-                main += closing_steps[0:1] + [step]
-                closing_steps = closing_steps[1:]
+            main = first + second[0:1]
             main.append(lambda: clamp_on_vector(b, 0))
             main += second[1:] + tasks[0:1]
             main.append(lambda: clamp_on_vector(b, 1))
             main += tasks[1:]
+            for i, step in enumerate(closing_steps):
+                main.insert(CLOSE_FROM + 2 * i, step)
             run(main, [lambda: None] * SMALL_FROM + small)
             for pair in range(CH // PAIR):
                 multiply(b, pair, OWN)
@@ -668,41 +695,52 @@ def tile_tokenmudule_pa_s_kernel(tc, patch_tokens, fc1_w, fc1_b, out):
         b = B - 1
         for pair in range(CH // PAIR):
             scale_cubes(b, pair)
-            steps = product_steps(b, pair)
-            run(steps[0 : vector_clamps(b)], [])
+        for pair in range(CH // PAIR):
             multiply(b, pair, OWN)
             clamp(b, pair, OWN)
-            run(steps[vector_clamps(b) :], [])
-            clamp_on_vector(b, pair)
-            for k in range(vector_clamps(b), OWN):
-                clamp(b, pair, k)
-            window_sum(b, pair)
-        for task in add_x_tasks(round_ending(b - 2)):
-            task()
-        square_sums_on_vector(round_ending(b - 2))
-        newton_roots(round_ending(b - 2))
-        for task in scale_tokens_tasks(round_ending(b - 2), inverse=False):
+        tasks = add_x_tasks(round_ending(b - 2))
+        previous = ()
+        for ch in range(CH):
+            for k in range(OWN):
+                multiply_chunk(b, ch, k)
+                if k == 0:
+                    for c in previous:
+                        clamp_chunk(b, c)
+                        window_chunk(b, c)
+            previous = (ch,)
+            if ch == 2:
+                for task in tasks:
+                    task()
+        square_sums(round_ending(b - 2))
+        roots(round_ending(b - 2))
+        for c in previous:
+            clamp_chunk(b, c)
+            window_chunk(b, c)
+        for task in scale_tokens_tasks(round_ending(b - 2)):
             task()
         log_sum((b - 1, b))
+        turn_tokens(round_ending(b - 2), on_vector=True)
+        for image in round_ending(b - 2):
+            project_one(image)
         exp_sum((b, b - 1))
+        for image in round_ending(b - 2):
+            add_bias(image)
         preload(ACT.Sqrt)
-        turn_tokens(round_ending(b - 2))
         for image in (b, b - 1):
             for task in add_x_tasks((image,)):
                 task()
             square_sums_split(image)
-        project(round_ending(b - 2))
         roots((b, b - 1))
         preload(ACT.Gelu)
         for image in (b, b - 1):
             for task in scale_tokens_tasks((image,)):
                 task()
-            turn_tokens((image,))
+        turn_tokens((b,), on_vector=True)
+        for first in range(0, B - 2, 2):
+            finish((first, first + 1))
+        turn_tokens((b - 1,))
         for image in (b, b - 1):
-            project((image,))
-
-        stored = out.rearrange("b (h p) f -> p b h f", p=P)
-        for first in range(0, B, 2):
-            images = slice(first, first + 2)
-            nc.scalar.activation(out=result[:, images], in_=pre_act[:, images], func=ACT.Gelu)
-            nc.sync.dma_start(out=stored[:, images], in_=result[:, images])
+            project_one(image)
+        for image in (b, b - 1):
+            add_bias(image)
+            finish((image,))

@@ -32,6 +32,7 @@ V_CLAMPS = 3
 V_CLAMPS_LAST = 4
 V_CLAMPS_EVEN = 1
 SMALL_FROM = 5
+HEAD_FROM = 5
 CLOSE_FROM = 2
 K_LEFT = OFFSETS.index((0, -1))
 TERMS = [(k, 0) for k in range(K)] + [(K_LEFT, 1)]
@@ -65,7 +66,8 @@ def tile_tokenmudule_pa_s_kernel(tc, patch_tokens, fc1_w, fc1_b, out):
             return ctx.enter_context(tc.psum_pool(name=name, bufs=bufs))
 
         keep = sbuf("keep", 1)
-        nat_pool = sbuf("nat", 2)
+        nat_pool = sbuf("nat", B)
+        head_pool = sbuf("head", 2)
         q_pool = sbuf("q", 3)
         unread_pool = sbuf("unread", 4)
         coef_pool = sbuf("coef", 3)
@@ -96,7 +98,7 @@ def tile_tokenmudule_pa_s_kernel(tc, patch_tokens, fc1_w, fc1_b, out):
         nc.vector.memset(minus_eps[:], -EPS_GEM_CUBED)
 
         p_pad = keep.tile([P, 2, CH, PADDED], F32)
-        nc.gpsimd.memset(p_pad[:], 0.0)
+        nc.vector.memset(p_pad[:], 0.0)
         term_tiles = [
             keep.tile([P, K, PAIR, TERM_COLS], F32, name="terms%d" % i) for i in range(TERM_TILES)
         ]
@@ -111,6 +113,7 @@ def tile_tokenmudule_pa_s_kernel(tc, patch_tokens, fc1_w, fc1_b, out):
         one = keep.tile([P, 1], F32)
         nc.vector.memset(one[:], 1.0)
         unused = keep.tile([P, 1], F32)
+        norm_sq_head = keep.tile([P, OWN - HEAD_FROM, CH], F32)
         own_sq = keep.tile([P, B, CH], F32)
         pre_act = keep.tile([P, B, H, F], F32)
         result = keep.tile([P, B, H, F], F32)
@@ -205,9 +208,14 @@ def tile_tokenmudule_pa_s_kernel(tc, patch_tokens, fc1_w, fc1_b, out):
         def start_coefficients(b):
             floored = coef_pool.tile([P, K, CH], F32, name="n_floored")
             nc.vector.tensor_scalar_max(floored[:, OWN, :], own_sq[:, b, :], EPS_NORM_SQUARED)
+            summed = HEAD_FROM if b == 0 else OWN
             nc.vector.tensor_scalar_max(
-                floored[:, 0:OWN, :], norm_sq[b][:, 0:OWN, :], EPS_NORM_SQUARED
+                floored[:, 0:summed, :], norm_sq[b][:, 0:summed, :], EPS_NORM_SQUARED
             )
+            if b == 0:
+                nc.vector.tensor_scalar_max(
+                    floored[:, HEAD_FROM:OWN, :], norm_sq_head[:], EPS_NORM_SQUARED
+                )
             norm[b] = coef_pool.tile([P, K, CH], F32, name="norm")
             nc.scalar.activation(out=norm[b][:], in_=floored[:], func=ACT.Sqrt)
 
@@ -583,11 +591,9 @@ def tile_tokenmudule_pa_s_kernel(tc, patch_tokens, fc1_w, fc1_b, out):
                     return images
             return ()
 
-        def norms(b, half, extra):
-            for k in range(OWN):
+        def norms(b, half, offsets=range(OWN)):
+            for k in offsets:
                 sum_products(b, k, half)
-                for step in extra[k : k + 1]:
-                    step()
 
         def preload(func):
             nc.scalar.activation(out=unused[:], in_=one[:], func=func)
@@ -626,19 +632,52 @@ def tile_tokenmudule_pa_s_kernel(tc, patch_tokens, fc1_w, fc1_b, out):
                     clamp(b, pair, k)
                 window_sum(b, pair)
 
+        def head_products(b, k):
+            di, dj = OFFSETS[k]
+            top = -di
+            lo, hi = max(0, -dj), GRID - max(0, dj)
+            rows, cols = GRID - top, hi - lo
+            grids = q[b][:].rearrange("p c (i j) -> p c i j", j=GRID)
+            products = head_pool.tile([P, CH, T], F32, name="head")
+            for pair in range(CH // PAIR):
+                chunks = slice(pair * PAIR, (pair + 1) * PAIR)
+                nc.gpsimd.tensor_tensor(
+                    out=products[:, chunks, 0 : rows * cols].rearrange(
+                        "p c (i j) -> p c i j", j=cols
+                    ),
+                    in0=grids[:, chunks, top:GRID, lo:hi],
+                    in1=grids[:, chunks, 0:rows, lo + dj : hi + dj],
+                    op=ALU.mult,
+                )
+                for ch in range(pair * PAIR, (pair + 1) * PAIR):
+                    unread = unread_pool.tile([P, T], BF16, name="unread_s")
+                    nc.scalar.activation(
+                        out=unread[:, 0 : rows * cols],
+                        in_=products[:, ch, 0 : rows * cols],
+                        func=ACT.Copy,
+                        accum_out=norm_sq_head[:, k - HEAD_FROM, ch : ch + 1],
+                    )
+
+        preload(ACT.Sqrt)
         square_x(0, 4)
         transpose_q(0, 0)
         copy_q(0, 0)
         transpose_q(0, 1)
-        copy_q(0, 1, on_vector=True)
+        copy_q(0, 1)
         square_x(1)
         transpose_x(0)
-        for half in range(2):
-            norms(0, half, [])
-            sum_squares(0, half)
-            transpose_q(1, half)
-            if half == 0:
-                copy_q(1, half)
+        sum_squares(0, 0)
+        sum_squares(0, 1)
+        square_x(2)
+        for k in range(HEAD_FROM, OWN):
+            head_products(0, k)
+            if k == HEAD_FROM:
+                norms(0, 0, range(HEAD_FROM))
+                transpose_q(1, 0)
+                copy_q(1, 0)
+        square_x(3)
+        norms(0, 1, range(HEAD_FROM))
+        transpose_q(1, 1)
         nc.vector.tensor_copy(out=w_grouped[:], in_=w_raw[:].rearrange("p t f -> p f t"))
         nc.vector.quantize_mx(
             out=w_codes[:].bitcast(FP8X4),
@@ -650,22 +689,22 @@ def tile_tokenmudule_pa_s_kernel(tc, patch_tokens, fc1_w, fc1_b, out):
         for b in range(-1, B - 2):
             small = coefficient_steps(b + 1)
             tasks = add_x_tasks(round_ending(b - 1)) + scale_tokens_tasks(round_ending(b - 2))
+            copy_q(b + 2, 1)
             if b >= 0:
                 transpose_x(b + 1)
                 vector_phase(b, small, tasks, round_ending(b - 3))
-            copy_q(b + 2, 1)
             for half in range(2):
                 sum_squares(b + 2, half)
-            if b + 3 < B:
-                square_x(b + 3)
             if b < 0:
+                for image in range(4, B):
+                    square_x(image)
                 run([], small)
             if b + 1 < B:
                 for pair in range(CH // PAIR):
                     scale_cubes(b + 1, pair)
                     gpsimd_products(b + 1, pair)
             if b + 2 < B:
-                norms(b + 2, 0, [])
+                norms(b + 2, 0)
                 if b + 3 < B:
                     transpose_q(b + 3, 0)
             square_sums(round_ending(b - 1))
@@ -678,7 +717,7 @@ def tile_tokenmudule_pa_s_kernel(tc, patch_tokens, fc1_w, fc1_b, out):
             exp_sum(summed)
             turn_tokens(round_ending(b - 2))
             if b + 2 < B:
-                norms(b + 2, 1, [])
+                norms(b + 2, 1)
                 if b + 3 < B:
                     transpose_q(b + 3, 1)
             if b + 2 < B:

@@ -31,9 +31,10 @@ ON_V = 3
 V_CLAMPS = 3
 V_CLAMPS_LAST = 4
 V_CLAMPS_EVEN = 1
-SMALL_FROM = 5
+SMALL_FROM = 6
 HEAD_FROM = 5
-CLOSE_FROM = 2
+CLOSE_FROM = 3
+BIAS_FROM = 9
 K_LEFT = OFFSETS.index((0, -1))
 TERMS = [(k, 0) for k in range(K)] + [(K_LEFT, 1)]
 
@@ -97,8 +98,11 @@ def tile_tokenmudule_pa_s_kernel(tc, patch_tokens, fc1_w, fc1_b, out):
         minus_eps = keep.tile([P, 1], F32)
         nc.vector.memset(minus_eps[:], -EPS_GEM_CUBED)
 
+        one = keep.tile([P, 1], F32)
+        nc.vector.memset(one[:], 1.0)
+        unused = keep.tile([P, 1], F32)
         p_pad = keep.tile([P, 2, CH, PADDED], F32)
-        nc.vector.memset(p_pad[:], 0.0)
+        nc.vector.memset(p_pad[:, 0], 0.0)
         term_tiles = [
             keep.tile([P, K, PAIR, TERM_COLS], F32, name="terms%d" % i) for i in range(TERM_TILES)
         ]
@@ -110,9 +114,6 @@ def tile_tokenmudule_pa_s_kernel(tc, patch_tokens, fc1_w, fc1_b, out):
         w_codes = keep.tile([P, F], U32, align_bytes=64)
         w_scales = keep.tile([P, F], U8, align_bytes=64)
 
-        one = keep.tile([P, 1], F32)
-        nc.vector.memset(one[:], 1.0)
-        unused = keep.tile([P, 1], F32)
         norm_sq_head = keep.tile([P, OWN - HEAD_FROM, CH], F32)
         own_sq = keep.tile([P, B, CH], F32)
         pre_act = keep.tile([P, B, H, F], F32)
@@ -148,13 +149,35 @@ def tile_tokenmudule_pa_s_kernel(tc, patch_tokens, fc1_w, fc1_b, out):
                         ident_bf[:],
                     )
 
-        def square_x(b, pieces=1):
+        def square_x(b):
             q_nat[b] = nat_pool.tile([P, H, C], F32, name="q_nat")
-            for i in range(pieces):
-                cols = slice(i * C // pieces, (i + 1) * C // pieces)
-                nc.scalar.activation(
-                    out=q_nat[b][:, :, cols], in_=x_nat[:, b, :, cols], func=ACT.Square
-                )
+            nc.scalar.activation(out=q_nat[b][:], in_=x_nat[:, b], func=ACT.Square)
+
+        def square_by_chunks(b):
+            q_nat[b] = nat_pool.tile([P, H, C], F32, name="q_nat")
+            for ch in range(CH):
+                cols = slice(ch * P, (ch + 1) * P)
+                if ch % 2 == 0:
+                    nc.scalar.activation(
+                        out=q_nat[b][:, :, cols], in_=x_nat[:, b, :, cols], func=ACT.Square
+                    )
+                else:
+                    nc.vector.tensor_tensor(
+                        out=q_nat[b][:, :, cols],
+                        in0=x_nat[:, b, :, cols],
+                        in1=x_nat[:, b, :, cols],
+                        op=ALU.mult,
+                    )
+
+        def copy_by_chunks(b, half):
+            if half == 0:
+                q[b] = q_pool.tile([P, CH, T], F32, name="q")
+            for c in range(PAIR):
+                copied = q[b][:, half * PAIR + c, :]
+                if c == 0:
+                    nc.scalar.copy(out=copied, in_=qT[b, half][:, c, :])
+                else:
+                    nc.vector.tensor_copy(out=copied, in_=qT[b, half][:, c, :])
 
         def transpose_q(b, half):
             qT[b, half] = qT_psum.tile([P, PAIR, T], F32, name="qT")
@@ -525,7 +548,9 @@ def tile_tokenmudule_pa_s_kernel(tc, patch_tokens, fc1_w, fc1_b, out):
         def turn_tokens(images, on_vector=False):
             for b in images:
                 words = closing[b, "tokens"][:].rearrange("p h c -> p (h c)").bitcast(F32)
-                if b < B - 4 or b % 2 == 0:
+                if b < ROUND:
+                    tokT = acc_psum.tile([P, H, 2, P], F32, name="acc")
+                elif b < B - 4 or b % 2 == 0:
                     tokT = proj_psum.tile([P, H, 2, P], F32, name="proj")
                 else:
                     tokT = xT_psum.tile([P, H, 2, P], F32, name="xT")
@@ -544,26 +569,23 @@ def tile_tokenmudule_pa_s_kernel(tc, patch_tokens, fc1_w, fc1_b, out):
                     in_=tokT[:].rearrange("p h u r -> p h r u"),
                 )
 
-        def project(images):
-            for b in images:
-                project_one(b)
-                add_bias(b)
+        def project_steps(images):
+            products = {}
 
-        def project_one(b):
-            if True:
+            def quantise(b):
+                if b == images[0]:
+                    if b == B - 1:
+                        products[0] = xT_psum.tile([P, 1, H, F], F32, name="xT")
+                    else:
+                        products[0] = proj_psum.tile([P, len(images), H, F], F32, name="proj")
                 codes = tail_pool.tile([P, H * P], U32, name="codes", align_bytes=64)
                 scales = tail_pool.tile([P, H * P], U8, name="scales", align_bytes=64)
                 nc.vector.quantize_mx(
                     out=codes[:].bitcast(FP8X4), scales=scales[:], in_=closing[b, "grouped"][:]
                 )
-                if b < B - 4 or b % 2 == 0:
-                    product = proj_psum.tile([P, H, F], F32, name="proj")
-                else:
-                    product = xT_psum.tile([P, H, F], F32, name="xT")
-                closing[b, "product"] = product
                 for h in range(H):
                     nc.tensor.matmul_mx(
-                        out=product[:, h, :],
+                        out=products[0][:, b - images[0], h, :],
                         lhsT=codes[:, h * P : (h + 1) * P].bitcast(FP8X4),
                         lhsT_scale=scales[:, h * P : (h + 1) * P],
                         rhs=w_codes[:].bitcast(FP8X4),
@@ -572,14 +594,17 @@ def tile_tokenmudule_pa_s_kernel(tc, patch_tokens, fc1_w, fc1_b, out):
                         stop=True,
                     )
 
-        def add_bias(b):
-            if True:
+            def add_bias():
                 nc.vector.tensor_tensor(
-                    out=pre_act[:, b],
-                    in0=closing[b, "product"][:],
-                    in1=bias[:].unsqueeze(1).to_broadcast([P, H, F]),
+                    out=pre_act[:, images[0] : images[-1] + 1],
+                    in0=products[0][:],
+                    in1=bias[:].unsqueeze(1).unsqueeze(1).to_broadcast([P, len(images), H, F]),
                     op=ALU.add,
                 )
+
+            if not images:
+                return []
+            return [lambda b=b: quantise(b) for b in images] + [add_bias]
 
         def gpsimd_products(b, pair):
             for k in range(on_vector_count(b), OWN):
@@ -612,17 +637,14 @@ def tile_tokenmudule_pa_s_kernel(tc, patch_tokens, fc1_w, fc1_b, out):
 
         def vector_phase(b, small, tasks, quantised):
             first, second = product_steps(b, 0), product_steps(b, 1)
-            closing_steps = []
-            for image in quantised:
-                closing_steps.append(lambda image=image: project_one(image))
-                closing_steps.append(lambda image=image: add_bias(image))
+            closing_steps = project_steps(quantised)
             main = first + second[0:1]
             main.append(lambda: clamp_on_vector(b, 0))
             main += second[1:] + tasks[0:1]
             main.append(lambda: clamp_on_vector(b, 1))
             main += tasks[1:]
             for i, step in enumerate(closing_steps):
-                main.insert(CLOSE_FROM + 2 * i, step)
+                main.insert(CLOSE_FROM + i if i < ROUND else BIAS_FROM, step)
             run(main, [lambda: None] * SMALL_FROM + small)
             for pair in range(CH // PAIR):
                 multiply(b, pair, OWN)
@@ -659,7 +681,7 @@ def tile_tokenmudule_pa_s_kernel(tc, patch_tokens, fc1_w, fc1_b, out):
                     )
 
         preload(ACT.Sqrt)
-        square_x(0, 4)
+        square_by_chunks(0)
         transpose_q(0, 0)
         copy_q(0, 0)
         transpose_q(0, 1)
@@ -676,6 +698,7 @@ def tile_tokenmudule_pa_s_kernel(tc, patch_tokens, fc1_w, fc1_b, out):
                 transpose_q(1, 0)
                 copy_q(1, 0)
         square_x(3)
+        nc.gpsimd.memset(p_pad[:, 1], 0.0)
         norms(0, 1, range(HEAD_FROM))
         transpose_q(1, 1)
         nc.vector.tensor_copy(out=w_grouped[:], in_=w_raw[:].rearrange("p t f -> p f t"))
@@ -759,11 +782,11 @@ def tile_tokenmudule_pa_s_kernel(tc, patch_tokens, fc1_w, fc1_b, out):
             task()
         log_sum((b - 1, b))
         turn_tokens(round_ending(b - 2), on_vector=True)
-        for image in round_ending(b - 2):
-            project_one(image)
+        steps = project_steps(round_ending(b - 2))
+        for step in steps[0:-1]:
+            step()
         exp_sum((b, b - 1))
-        for image in round_ending(b - 2):
-            add_bias(image)
+        steps[-1]()
         preload(ACT.Sqrt)
         for image in (b, b - 1):
             for task in add_x_tasks((image,)):
@@ -778,8 +801,10 @@ def tile_tokenmudule_pa_s_kernel(tc, patch_tokens, fc1_w, fc1_b, out):
         for first in range(0, B - 2, 2):
             finish((first, first + 1))
         turn_tokens((b - 1,))
-        for image in (b, b - 1):
-            project_one(image)
-        for image in (b, b - 1):
-            add_bias(image)
-            finish((image,))
+        last, other = project_steps((b,)), project_steps((b - 1,))
+        last[0]()
+        other[0]()
+        last[1]()
+        finish((b,))
+        other[1]()
+        finish((b - 1,))

@@ -5,7 +5,6 @@ from concourse.masks import make_identity
 
 F32 = mybir.dt.float32
 BF16 = mybir.dt.bfloat16
-I32 = mybir.dt.int32
 U32 = mybir.dt.uint32
 U8 = mybir.dt.uint8
 FP8X4 = mybir.dt.float8_e4m3fn_x4
@@ -19,6 +18,8 @@ T = GRID * GRID
 H = T // P
 C = 512
 CH = C // P
+PAIR = 2
+PAIRS = CH // PAIR
 F = 128
 PACK = 4
 
@@ -27,29 +28,28 @@ FLOPS = 2 * B * T * C * F
 OFFSETS = [(0, -1), (-1, 0), (-1, -1), (-1, 1), (-2, -1), (-2, 0), (-2, 1), (0, 0)]
 K = len(OFFSETS)
 OWN = OFFSETS.index((0, 0))
-ON_V = 3
-V_CLAMPS = 3
-V_CLAMPS_LAST = 4
-V_CLAMPS_EVEN = 1
-SMALL_FROM = 6
-HEAD_FROM = 5
-CLOSE_FROM = 3
-BIAS_FROM = 9
 K_LEFT = OFFSETS.index((0, -1))
 TERMS = [(k, 0) for k in range(K)] + [(K_LEFT, 1)]
-
 MAX_TOP = 2
+
+ON_V = 3
+V_CLAMPS_EVEN = 1
+HEAD_FROM = 5
+
+SMALL_FROM = 6
+CLOSE_FROM = 3
+BIAS_FROM = 9
+
 LEAD = 4
 ROW = LEAD + GRID
 PADDED = GRID * ROW + 8
 TERM_COLS = T + 8
+TERM_TILES = 5
 
 EPS_GEM_CUBED = 1e-18
 EPS_NORM_SQUARED = 1e-24
-RSQRT_BITS = 0x5F3759DF
+RATIO_SQUARED_MAX = 1e22
 
-TERM_TILES = 5
-PAIR = 2
 ROUNDS = [(0, 1), (2, 3), (4, 5), (6,), (7,)]
 ROUND = 2
 
@@ -75,15 +75,18 @@ def tile_tokenmudule_pa_s_kernel(tc, patch_tokens, fc1_w, fc1_b, out):
         pooled_pool = sbuf("pooled", 2 * ROUND)
         tail_pool = sbuf("tail", 2 * ROUND)
         xT_psum = psum("xT_psum", 1)
-        qT_psum = psum("qT_psum", CH // PAIR)
+        qT_psum = psum("qT_psum", PAIRS)
         acc_psum = psum("acc_psum", ROUND * H)
         proj_psum = psum("proj_psum", 1)
 
         x_nat = keep.tile([P, B, H, C], BF16)
         for b in range(B):
-            nc.sync.dma_start(
-                out=x_nat[:, b], in_=patch_tokens[b].rearrange("(h p) c -> p h c", p=P)
-            )
+            halves_of_b = patch_tokens[b].rearrange("(h p) c -> p h c", p=P)
+            if b == 0:
+                nc.sync.dma_start(out=x_nat[:, b, 0], in_=halves_of_b[:, 0])
+                nc.scalar.dma_start(out=x_nat[:, b, 1], in_=halves_of_b[:, 1])
+            else:
+                nc.sync.dma_start(out=x_nat[:, b], in_=halves_of_b)
         w_raw = keep.tile([P, PACK, F], BF16)
         nc.scalar.dma_start(out=w_raw[:], in_=fc1_w.rearrange("(p t) f -> p t f", t=PACK))
         bias = keep.tile([P, F], BF16)
@@ -97,10 +100,10 @@ def tile_tokenmudule_pa_s_kernel(tc, patch_tokens, fc1_w, fc1_b, out):
         nc.vector.memset(plus_eps[:], EPS_GEM_CUBED)
         minus_eps = keep.tile([P, 1], F32)
         nc.vector.memset(minus_eps[:], -EPS_GEM_CUBED)
-
         one = keep.tile([P, 1], F32)
         nc.vector.memset(one[:], 1.0)
         unused = keep.tile([P, 1], F32)
+
         p_pad = keep.tile([P, 2, CH, PADDED], F32)
         nc.vector.memset(p_pad[:, 0], 0.0)
         term_tiles = [
@@ -113,14 +116,13 @@ def tile_tokenmudule_pa_s_kernel(tc, patch_tokens, fc1_w, fc1_b, out):
         w_grouped = keep.tile([P, F, PACK], BF16, align_bytes=64)
         w_codes = keep.tile([P, F], U32, align_bytes=64)
         w_scales = keep.tile([P, F], U8, align_bytes=64)
-
         norm_sq_head = keep.tile([P, OWN - HEAD_FROM, CH], F32)
         own_sq = keep.tile([P, B, CH], F32)
         pre_act = keep.tile([P, B, H, F], F32)
         result = keep.tile([P, B, H, F], F32)
 
-        xT = {}
         q_nat = {}
+        xT = {}
         qT = {}
         q = {}
         norm_sq = {}
@@ -129,15 +131,41 @@ def tile_tokenmudule_pa_s_kernel(tc, patch_tokens, fc1_w, fc1_b, out):
         coef = {}
         acc = {}
         pooled = {}
-        closing = {}
+        r_sq, r_norm = {}, {}
+        tokens = {}
+        grouped = {}
+
+        def preload(func):
+            nc.scalar.activation(out=unused[:], in_=one[:], func=func)
+
+        def round_ending(b):
+            for images in ROUNDS:
+                if images[-1] == b:
+                    return images
+            return ()
 
         def grid(ap):
             return ap.rearrange("p (i j) -> p i j", j=GRID)
 
-        def padded_rows(b, chunks, dj):
-            first = LEAD + dj
-            flat = p_pad[:, b % 2, chunks, first : first + GRID * ROW]
-            return flat.rearrange("p c (i j) -> p c i j", j=ROW)[:, :, :, 0:GRID]
+        def grids(ap):
+            return ap.rearrange("p c (i j) -> p c i j", j=GRID)
+
+        def chunks_of(pair):
+            return range(pair * PAIR, (pair + 1) * PAIR)
+
+        def square_x(b):
+            q_nat[b] = nat_pool.tile([P, H, C], F32, name="q_nat")
+            nc.scalar.activation(out=q_nat[b][:], in_=x_nat[:, b], func=ACT.Square)
+
+        def square_first(b):
+            q_nat[b] = nat_pool.tile([P, H, C], F32, name="q_nat")
+            for ch in range(CH):
+                square = q_nat[b][:, :, ch * P : (ch + 1) * P]
+                x = x_nat[:, b, :, ch * P : (ch + 1) * P]
+                if ch % 2 == 0:
+                    nc.scalar.activation(out=square, in_=x, func=ACT.Square)
+                else:
+                    nc.vector.tensor_tensor(out=square, in0=x, in1=x, op=ALU.mult)
 
         def transpose_x(b):
             xT[b] = xT_psum.tile([P, CH, T], BF16, name="xT")
@@ -149,58 +177,23 @@ def tile_tokenmudule_pa_s_kernel(tc, patch_tokens, fc1_w, fc1_b, out):
                         ident_bf[:],
                     )
 
-        def square_x(b):
-            q_nat[b] = nat_pool.tile([P, H, C], F32, name="q_nat")
-            nc.scalar.activation(out=q_nat[b][:], in_=x_nat[:, b], func=ACT.Square)
-
-        def square_by_chunks(b):
-            q_nat[b] = nat_pool.tile([P, H, C], F32, name="q_nat")
-            for ch in range(CH):
-                cols = slice(ch * P, (ch + 1) * P)
-                if ch % 2 == 0:
-                    nc.scalar.activation(
-                        out=q_nat[b][:, :, cols], in_=x_nat[:, b, :, cols], func=ACT.Square
-                    )
-                else:
-                    nc.vector.tensor_tensor(
-                        out=q_nat[b][:, :, cols],
-                        in0=x_nat[:, b, :, cols],
-                        in1=x_nat[:, b, :, cols],
-                        op=ALU.mult,
-                    )
-
-        def copy_by_chunks(b, half):
-            if half == 0:
-                q[b] = q_pool.tile([P, CH, T], F32, name="q")
-            for c in range(PAIR):
-                copied = q[b][:, half * PAIR + c, :]
-                if c == 0:
-                    nc.scalar.copy(out=copied, in_=qT[b, half][:, c, :])
-                else:
-                    nc.vector.tensor_copy(out=copied, in_=qT[b, half][:, c, :])
-
-        def transpose_q(b, half):
-            qT[b, half] = qT_psum.tile([P, PAIR, T], F32, name="qT")
-            for c in range(PAIR):
-                ch = half * PAIR + c
+        def transpose_q(b, pair):
+            qT[b, pair] = qT_psum.tile([P, PAIR, T], F32, name="qT")
+            for ch in chunks_of(pair):
                 for h in range(H):
                     nc.tensor.transpose(
-                        qT[b, half][:, c, h * P : (h + 1) * P],
+                        qT[b, pair][:, ch % PAIR, h * P : (h + 1) * P],
                         q_nat[b][:, h, ch * P : (ch + 1) * P],
                         ident_f[:],
                     )
 
-        def copy_q(b, half, on_vector=False):
-            if half == 0:
+        def copy_q(b, pair):
+            if pair == 0:
                 q[b] = q_pool.tile([P, CH, T], F32, name="q")
-            copied = q[b][:, half * PAIR : (half + 1) * PAIR, :]
-            if on_vector:
-                nc.vector.tensor_copy(out=copied, in_=qT[b, half][:])
-            else:
-                nc.scalar.copy(out=copied, in_=qT[b, half][:])
+            nc.scalar.copy(out=q[b][:, pair * PAIR : (pair + 1) * PAIR, :], in_=qT[b, pair][:])
 
-        def sum_squares(b, half):
-            for ch in range(half * PAIR, (half + 1) * PAIR):
+        def sum_squares(b, pair):
+            for ch in chunks_of(pair):
                 unread = unread_pool.tile([P, T], BF16, name="unread_s")
                 nc.scalar.activation(
                     out=unread[:],
@@ -209,36 +202,63 @@ def tile_tokenmudule_pa_s_kernel(tc, patch_tokens, fc1_w, fc1_b, out):
                     accum_out=own_sq[:, b, ch : ch + 1],
                 )
 
-        def sum_products(b, k, half):
+        def overlap(k):
+            di, dj = OFFSETS[k]
+            lo, hi = max(0, -dj), GRID - max(0, dj)
+            here = (slice(-di, GRID), slice(lo, hi))
+            there = (slice(0, GRID + di), slice(lo + dj, hi + dj))
+            return here, there, GRID + di, hi - lo
+
+        def sum_products(b, pair, offsets=range(OWN)):
             if b not in norm_sq:
                 norm_sq[b] = coef_pool.tile([P, K, CH], F32, name="norm_sq")
-            di, dj = OFFSETS[k]
-            top = -di
-            lo, hi = max(0, -dj), GRID - max(0, dj)
-            rows, cols = GRID - top, hi - lo
-            for ch in range(half * PAIR, (half + 1) * PAIR):
-                unread = unread_pool.tile([P, T], F32, name="unread_v")
-                nc.vector.scalar_tensor_tensor(
-                    out=unread[:, 0 : rows * cols].rearrange("p (i j) -> p i j", j=cols),
-                    in0=grid(qT[b, half][:, ch % PAIR, :])[:, top:GRID, lo:hi],
-                    scalar=1.0,
-                    in1=grid(q[b][:, ch, :])[:, 0:rows, lo + dj : hi + dj],
-                    op0=ALU.mult,
-                    op1=ALU.mult,
-                    accum_out=norm_sq[b][:, k, ch : ch + 1],
-                )
+            for k in offsets:
+                here, there, rows, cols = overlap(k)
+                for ch in chunks_of(pair):
+                    unread = unread_pool.tile([P, T], F32, name="unread_v")
+                    nc.vector.scalar_tensor_tensor(
+                        out=unread[:, 0 : rows * cols].rearrange("p (i j) -> p i j", j=cols),
+                        in0=grid(qT[b, pair][:, ch % PAIR, :])[:, here[0], here[1]],
+                        scalar=1.0,
+                        in1=grid(q[b][:, ch, :])[:, there[0], there[1]],
+                        op0=ALU.mult,
+                        op1=ALU.mult,
+                        accum_out=norm_sq[b][:, k, ch : ch + 1],
+                    )
 
-        def start_coefficients(b):
-            floored = coef_pool.tile([P, K, CH], F32, name="n_floored")
-            nc.vector.tensor_scalar_max(floored[:, OWN, :], own_sq[:, b, :], EPS_NORM_SQUARED)
-            summed = HEAD_FROM if b == 0 else OWN
-            nc.vector.tensor_scalar_max(
-                floored[:, 0:summed, :], norm_sq[b][:, 0:summed, :], EPS_NORM_SQUARED
-            )
-            if b == 0:
-                nc.vector.tensor_scalar_max(
-                    floored[:, HEAD_FROM:OWN, :], norm_sq_head[:], EPS_NORM_SQUARED
+        def sum_without_vector(b, k):
+            here, there, rows, cols = overlap(k)
+            products = head_pool.tile([P, CH, T], F32, name="head")
+            for pair in range(PAIRS):
+                these = slice(pair * PAIR, (pair + 1) * PAIR)
+                nc.gpsimd.tensor_tensor(
+                    out=products[:, these, 0 : rows * cols].rearrange(
+                        "p c (i j) -> p c i j", j=cols
+                    ),
+                    in0=grids(q[b][:])[:, these, here[0], here[1]],
+                    in1=grids(q[b][:])[:, these, there[0], there[1]],
+                    op=ALU.mult,
                 )
+                for ch in chunks_of(pair):
+                    unread = unread_pool.tile([P, T], BF16, name="unread_s")
+                    nc.scalar.activation(
+                        out=unread[:, 0 : rows * cols],
+                        in_=products[:, ch, 0 : rows * cols],
+                        func=ACT.Copy,
+                        accum_out=norm_sq_head[:, k - HEAD_FROM, ch : ch + 1],
+                    )
+
+        def take_roots(b):
+            floored = coef_pool.tile([P, K, CH], F32, name="n_floored")
+            on_vector = HEAD_FROM if b == 0 else OWN
+            sums = [
+                (floored[:, OWN, :], own_sq[:, b, :]),
+                (floored[:, 0:on_vector, :], norm_sq[b][:, 0:on_vector, :]),
+            ]
+            if b == 0:
+                sums.append((floored[:, HEAD_FROM:OWN, :], norm_sq_head[:]))
+            for to, total in sums:
+                nc.vector.tensor_scalar_max(to, total, EPS_NORM_SQUARED)
             norm[b] = coef_pool.tile([P, K, CH], F32, name="norm")
             nc.scalar.activation(out=norm[b][:], in_=floored[:], func=ACT.Sqrt)
 
@@ -258,13 +278,23 @@ def tile_tokenmudule_pa_s_kernel(tc, patch_tokens, fc1_w, fc1_b, out):
                 lambda: nc.vector.tensor_tensor(
                     out=ratio_sq[:], in0=ratio[:], in1=ratio[:], op=ALU.mult
                 ),
-                lambda: nc.vector.tensor_tensor(
-                    out=coef[b][:], in0=ratio_sq[:], in1=inv_norm[b][:], op=ALU.mult
+                lambda: nc.vector.scalar_tensor_tensor(
+                    out=coef[b][:],
+                    in0=ratio_sq[:],
+                    scalar=RATIO_SQUARED_MAX,
+                    in1=inv_norm[b][:],
+                    op0=ALU.min,
+                    op1=ALU.mult,
                 ),
             ]
 
+        def padded_rows(b, chunks, dj):
+            first = LEAD + dj
+            flat = p_pad[:, b % 2, chunks, first : first + GRID * ROW]
+            return flat.rearrange("p c (i j) -> p c i j", j=ROW)[:, :, :, 0:GRID]
+
         def scale_cubes(b, pair):
-            for ch in range(pair * PAIR, (pair + 1) * PAIR):
+            for ch in chunks_of(pair):
                 nc.vector.scalar_tensor_tensor(
                     out=padded_rows(b, slice(ch, ch + 1), 0)[:, 0],
                     in0=grid(q[b][:, ch, :]),
@@ -275,96 +305,59 @@ def tile_tokenmudule_pa_s_kernel(tc, patch_tokens, fc1_w, fc1_b, out):
                 )
 
         def terms_of(b, pair):
-            return term_tiles[(b * (CH // PAIR) + pair) % TERM_TILES]
+            return term_tiles[(b * PAIRS + pair) % TERM_TILES]
 
-        def products_of(b, pair, k):
-            top = -OFFSETS[k][0]
-            return terms_of(b, pair)[:, k, :, top * GRID : T].rearrange(
-                "p c (i j) -> p c i j", j=GRID
+        def product_parts(b, pair, first, last, k):
+            di, dj = OFFSETS[k]
+            chunks = slice(pair * PAIR + first, pair * PAIR + last)
+            return (
+                grids(terms_of(b, pair)[:, k, first:last, -di * GRID : T]),
+                padded_rows(b, chunks, 0)[:, :, -di:GRID, :],
+                padded_rows(b, chunks, dj)[:, :, 0 : GRID + di, :],
             )
 
-        def on_vector_count(b):
-            return OWN if b == B - 1 else ON_V
-
-        def multiply(b, pair, k):
-            di, dj = OFFSETS[k]
-            top = -di
-            chunks = slice(pair * PAIR, (pair + 1) * PAIR)
-            products = products_of(b, pair, k)
-            here = padded_rows(b, chunks, 0)[:, :, top:GRID, :]
-            there = padded_rows(b, chunks, dj)[:, :, 0 : GRID - top, :]
-            if k == OWN:
-                nc.scalar.activation(out=products, in_=here, func=ACT.Square)
-            elif k < on_vector_count(b):
-                for c in range(PAIR):
-                    ch = pair * PAIR + c
-                    nc.vector.scalar_tensor_tensor(
-                        out=products[:, c],
-                        in0=here[:, c],
-                        scalar=coef[b][:, k, ch : ch + 1],
-                        in1=there[:, c],
-                        op0=ALU.mult,
-                        op1=ALU.mult,
-                    )
-            else:
-                nc.gpsimd.tensor_tensor(out=products, in0=here, in1=there, op=ALU.mult)
-
-        def multiply_chunk(b, ch, k):
-            di, dj = OFFSETS[k]
-            top = -di
-            chunk = slice(ch, ch + 1)
+        def multiply(b, ch, k):
+            c = ch % PAIR
+            product, here, there = product_parts(b, ch // PAIR, c, c + 1, k)
             nc.vector.scalar_tensor_tensor(
-                out=products_of(b, ch // PAIR, k)[:, ch % PAIR],
-                in0=padded_rows(b, chunk, 0)[:, 0, top:GRID, :],
+                out=product[:, 0],
+                in0=here[:, 0],
                 scalar=coef[b][:, k, ch : ch + 1],
-                in1=padded_rows(b, chunk, dj)[:, 0, 0 : GRID - top, :],
+                in1=there[:, 0],
                 op0=ALU.mult,
                 op1=ALU.mult,
             )
 
-        def clamp_chunk(b, ch):
-            term = terms_of(b, ch // PAIR)[:, 0:OWN, ch % PAIR, 0:T]
-            nc.vector.tensor_scalar(term, term, -EPS_GEM_CUBED, 0.0, op0=ALU.add, op1=ALU.max)
+        def multiply_on_gpsimd(b, pair):
+            for k in range(ON_V, OWN):
+                product, here, there = product_parts(b, pair, 0, PAIR, k)
+                nc.gpsimd.tensor_tensor(out=product, in0=here, in1=there, op=ALU.mult)
 
-        def clamp(b, pair, k):
-            top = -OFFSETS[k][0]
-            terms = terms_of(b, pair)
-            if k < on_vector_count(b):
-                term = terms[:, k, :, top * GRID : T]
-                nc.scalar.activation(out=term, in_=term, func=ACT.Relu, bias=minus_eps[:])
-            else:
-                for c in range(PAIR):
-                    ch = pair * PAIR + c
-                    term = terms[:, k, c, top * GRID : T]
-                    nc.scalar.activation(
-                        out=term,
-                        in_=term,
-                        func=ACT.Relu,
-                        scale=coef[b][:, k, ch : ch + 1],
-                        bias=minus_eps[:],
-                    )
+        def square_own(b, pair):
+            product, here, _ = product_parts(b, pair, 0, PAIR, OWN)
+            nc.scalar.activation(out=product, in_=here, func=ACT.Square)
 
-        def vector_clamps(b):
-            if b == B - 1:
-                return V_CLAMPS_LAST
-            return V_CLAMPS if b % 2 == 1 or b == B - 2 else V_CLAMPS_EVEN
+        def relu(terms, scale=1.0):
+            nc.scalar.activation(
+                out=terms, in_=terms, func=ACT.Relu, scale=scale, bias=minus_eps[:]
+            )
 
-        def clamp_on_vector(b, pair):
-            term = terms_of(b, pair)[:, 0 : vector_clamps(b), :, 0:T]
-            nc.vector.tensor_scalar(term, term, -EPS_GEM_CUBED, 0.0, op0=ALU.add, op1=ALU.max)
+        def clamp(b, ch, k):
+            terms = terms_of(b, ch // PAIR)[:, k, ch % PAIR, -OFFSETS[k][0] * GRID : T]
+            relu(terms, coef[b][:, k, ch : ch + 1])
 
-        def window_sum(b, pair):
-            for c in range(PAIR):
-                window_chunk(b, pair * PAIR + c)
+        def clamp_on_vector(b, pair, last, chunks=slice(0, PAIR)):
+            terms = terms_of(b, pair)[:, 0:last, chunks, 0:T]
+            nc.vector.tensor_scalar(terms, terms, -EPS_GEM_CUBED, 0.0, op0=ALU.add, op1=ALU.max)
 
-        def window_chunk(b, ch):
-            terms = terms_of(b, ch // PAIR)
+        def window_sum(b, ch):
             for h in range(H):
                 if (b, h) not in acc:
                     if b == B - 2:
                         acc[b, h] = qT_psum.tile([P, C], F32, name="qT")
                     else:
                         acc[b, h] = acc_psum.tile([P, C], F32, name="acc")
+            terms = terms_of(b, ch // PAIR)
             for i, (k, ahead) in enumerate(TERMS):
                 for h in range(H):
                     nc.tensor.matmul(
@@ -376,19 +369,8 @@ def tile_tokenmudule_pa_s_kernel(tc, patch_tokens, fc1_w, fc1_b, out):
                         stop=(i == len(TERMS) - 1),
                     )
 
-        stored = out.rearrange("b (h p) f -> p b h f", p=P)
-
-        def finish(images):
-            these = slice(images[0], images[-1] + 1)
-            nc.scalar.activation(out=result[:, these], in_=pre_act[:, these], func=ACT.Gelu)
-            nc.sync.dma_start(out=stored[:, these], in_=result[:, these])
-
         def halves(b):
             return [slice(0, 1), slice(1, 2)] if b >= B - 2 else [slice(0, 2)]
-
-        def pooled_of(images):
-            log_sum(images)
-            exp_sum(images)
 
         def log_sum(images):
             for b in images:
@@ -409,7 +391,7 @@ def tile_tokenmudule_pa_s_kernel(tc, patch_tokens, fc1_w, fc1_b, out):
                         out=pooled[b][:, h], in_=pooled[b][:, h], func=ACT.Exp, scale=1.0 / 3.0
                     )
 
-        def add_x_tasks(images):
+        def add_x_steps(images):
             return [
                 lambda b=b, h=h: nc.vector.tensor_tensor(
                     out=pooled[b][:, h], in0=pooled[b][:, h], in1=x_nat[:, b, h], op=ALU.add
@@ -418,137 +400,52 @@ def tile_tokenmudule_pa_s_kernel(tc, patch_tokens, fc1_w, fc1_b, out):
                 for h in halves(b)
             ]
 
-        def square_sums(images):
-            for b in images:
-                r_sq = tail_pool.tile([P, H], F32, name="r_sq")
-                closing[b, "r_sq"] = r_sq
-                for h in range(H):
-                    unread = unread_pool.tile([P, C], BF16, name="unread_r")
-                    nc.scalar.activation(
-                        out=unread[:],
-                        in_=pooled[b][:, h, :],
-                        func=ACT.Square,
-                        accum_out=r_sq[:, h : h + 1],
-                    )
+        def start_r_sums(b):
+            r_sq[b] = tail_pool.tile([P, H], F32, name="r_sq")
 
-        def square_sums_on_vector(images):
-            for b in images:
-                r_sq = tail_pool.tile([P, H], F32, name="r_sq")
-                closing[b, "r_sq"] = r_sq
-                for h in range(H):
-                    unread = unread_pool.tile([P, C], BF16, name="unread_r")
-                    nc.vector.scalar_tensor_tensor(
-                        out=unread[:],
-                        in0=pooled[b][:, h, :],
-                        scalar=1.0,
-                        in1=pooled[b][:, h, :],
-                        op0=ALU.mult,
-                        op1=ALU.mult,
-                        accum_out=r_sq[:, h : h + 1],
-                    )
-
-        def square_sums_split(b):
-            r_sq = tail_pool.tile([P, H], F32, name="r_sq")
-            closing[b, "r_sq"] = r_sq
+        def sum_r_squares(b, h, on_vector=False):
             unread = unread_pool.tile([P, C], BF16, name="unread_r")
-            nc.vector.scalar_tensor_tensor(
-                out=unread[:],
-                in0=pooled[b][:, 0, :],
-                scalar=1.0,
-                in1=pooled[b][:, 0, :],
-                op0=ALU.mult,
-                op1=ALU.mult,
-                accum_out=r_sq[:, 0:1],
-            )
-            unread = unread_pool.tile([P, C], BF16, name="unread_r")
-            nc.scalar.activation(
-                out=unread[:], in_=pooled[b][:, 1, :], func=ACT.Square, accum_out=r_sq[:, 1:2]
-            )
+            r, total = pooled[b][:, h, :], r_sq[b][:, h : h + 1]
+            if on_vector:
+                nc.vector.scalar_tensor_tensor(
+                    out=unread[:], in0=r, scalar=1.0, in1=r, op0=ALU.mult, op1=ALU.mult, accum_out=total
+                )
+            else:
+                nc.scalar.activation(out=unread[:], in_=r, func=ACT.Square, accum_out=total)
 
-        def roots(images):
+        def sum_round(images):
+            for b in images:
+                start_r_sums(b)
+                for h in range(H):
+                    sum_r_squares(b, h)
+
+        def take_r_roots(images):
             for b in images:
                 floored = tail_pool.tile([P, H], F32, name="r_floored")
-                nc.vector.tensor_scalar_max(floored[:], closing[b, "r_sq"][:], EPS_NORM_SQUARED)
-                r_norm = tail_pool.tile([P, H], F32, name="r_norm")
-                closing[b, "r_norm"] = r_norm
-                nc.scalar.activation(out=r_norm[:], in_=floored[:], func=ACT.Sqrt)
+                nc.vector.tensor_scalar_max(floored[:], r_sq[b][:], EPS_NORM_SQUARED)
+                r_norm[b] = tail_pool.tile([P, H], F32, name="r_norm")
+                nc.scalar.activation(out=r_norm[b][:], in_=floored[:], func=ACT.Sqrt)
 
-        def newton_roots(images):
+        def token_steps(images):
+            inverses, products = [], []
             for b in images:
-                m = tail_pool.tile([P, H], F32, name="rm")
-                seed = tail_pool.tile([P, H], I32, name="rseed")
-                t = tail_pool.tile([P, H], F32, name="rt")
-                u = tail_pool.tile([P, H], F32, name="ru")
-                y = tail_pool.tile([P, H], F32, name="inv_r")
-                closing[b, "inv_r"] = y
-                closing[b, "newton"] = (m, seed, t, u, y)
-
-            def on_all(step):
-                for b in images:
-                    step(*closing[b, "newton"], closing[b, "r_sq"])
-
-            V = nc.vector
-            on_all(lambda m, seed, t, u, y, r: V.tensor_scalar_max(m[:], r[:], EPS_NORM_SQUARED))
-            on_all(
-                lambda m, seed, t, u, y, r: V.tensor_single_scalar(
-                    seed[:], m[:].bitcast(I32), 1, ALU.logical_shift_right
+                inv_r = tail_pool.tile([P, H], F32, name="inv_r")
+                inverses.append(
+                    lambda b=b, inv_r=inv_r: nc.vector.reciprocal(inv_r[:], r_norm[b][:])
                 )
-            )
-            on_all(
-                lambda m, seed, t, u, y, r: V.tensor_scalar(
-                    seed[:], seed[:], -1.0, float(RSQRT_BITS), op0=ALU.mult, op1=ALU.add
-                )
-            )
-            for i in range(3):
-
-                def last(seed, y, i=i):
-                    return seed[:].bitcast(F32) if i == 0 else y[:]
-
-                on_all(
-                    lambda m, seed, t, u, y, r: V.scalar_tensor_tensor(
-                        out=t[:], in0=last(seed, y), scalar=1.0, in1=m[:], op0=ALU.mult, op1=ALU.mult
-                    )
-                )
-                on_all(
-                    lambda m, seed, t, u, y, r: V.scalar_tensor_tensor(
-                        out=u[:], in0=t[:], scalar=-0.5, in1=last(seed, y), op0=ALU.mult, op1=ALU.mult
-                    )
-                )
-                on_all(
-                    lambda m, seed, t, u, y, r: V.scalar_tensor_tensor(
-                        out=y[:], in0=u[:], scalar=1.5, in1=last(seed, y), op0=ALU.add, op1=ALU.mult
-                    )
-                )
-
-        def scale_tokens_tasks(images, inverse=True):
-            tasks = []
-            for b in images:
-                if inverse:
-                    inv_r = tail_pool.tile([P, H], F32, name="inv_r")
-                    closing[b, "inv_r"] = inv_r
-                tokens = tail_pool.tile([P, H, C], BF16, name="tokens")
-                closing[b, "tokens"] = tokens
-                if inverse:
-                    tasks.append(
-                        lambda b=b: nc.vector.reciprocal(
-                            closing[b, "inv_r"][:], closing[b, "r_norm"][:]
-                        )
-                    )
-            for b in images:
+                tokens[b] = tail_pool.tile([P, H, C], BF16, name="tokens")
                 for h in range(H):
-                    tasks.append(
-                        lambda b=b, h=h: nc.vector.tensor_scalar_mul(
-                            closing[b, "tokens"][:, h, :],
-                            pooled[b][:, h, :],
-                            closing[b, "inv_r"][:, h : h + 1],
+                    products.append(
+                        lambda b=b, h=h, inv_r=inv_r: nc.vector.tensor_scalar_mul(
+                            tokens[b][:, h, :], pooled[b][:, h, :], inv_r[:, h : h + 1]
                         )
                     )
-            return tasks
+            return inverses + products
 
         def turn_tokens(images, on_vector=False):
             for b in images:
-                words = closing[b, "tokens"][:].rearrange("p h c -> p (h c)").bitcast(F32)
-                if b < ROUND:
+                words = tokens[b][:].rearrange("p h c -> p (h c)").bitcast(F32)
+                if b in ROUNDS[0]:
                     tokT = acc_psum.tile([P, H, 2, P], F32, name="acc")
                 elif b < B - 4 or b % 2 == 0:
                     tokT = proj_psum.tile([P, H, 2, P], F32, name="proj")
@@ -561,31 +458,40 @@ def tile_tokenmudule_pa_s_kernel(tc, patch_tokens, fc1_w, fc1_b, out):
                             words[:, h * (C // 2) + u : (h + 1) * (C // 2) : 2],
                             ident_f[:],
                         )
-                grouped = tail_pool.tile([P, H * P * PACK], BF16, name="grouped", align_bytes=64)
-                closing[b, "grouped"] = grouped
+                grouped[b] = tail_pool.tile(
+                    [P, H * P * PACK], BF16, name="grouped", align_bytes=64
+                )
                 copy = nc.vector.tensor_copy if on_vector else nc.scalar.copy
                 copy(
-                    out=grouped[:].bitcast(F32).rearrange("p (h r u) -> p h r u", h=H, u=2),
+                    out=grouped[b][:].bitcast(F32).rearrange("p (h r u) -> p h r u", h=H, u=2),
                     in_=tokT[:].rearrange("p h u r -> p h r u"),
                 )
 
-        def project_steps(images):
-            products = {}
+        def quantise_weights():
+            nc.vector.tensor_copy(out=w_grouped[:], in_=w_raw[:].rearrange("p t f -> p f t"))
+            nc.vector.quantize_mx(
+                out=w_codes[:].bitcast(FP8X4),
+                scales=w_scales[:],
+                in_=w_grouped[:].rearrange("p f t -> p (f t)"),
+            )
+
+        def linear_steps(images):
+            product = {}
 
             def quantise(b):
                 if b == images[0]:
                     if b == B - 1:
-                        products[0] = xT_psum.tile([P, 1, H, F], F32, name="xT")
+                        product[0] = xT_psum.tile([P, 1, H, F], F32, name="xT")
                     else:
-                        products[0] = proj_psum.tile([P, len(images), H, F], F32, name="proj")
+                        product[0] = proj_psum.tile([P, len(images), H, F], F32, name="proj")
                 codes = tail_pool.tile([P, H * P], U32, name="codes", align_bytes=64)
                 scales = tail_pool.tile([P, H * P], U8, name="scales", align_bytes=64)
                 nc.vector.quantize_mx(
-                    out=codes[:].bitcast(FP8X4), scales=scales[:], in_=closing[b, "grouped"][:]
+                    out=codes[:].bitcast(FP8X4), scales=scales[:], in_=grouped[b][:]
                 )
                 for h in range(H):
                     nc.tensor.matmul_mx(
-                        out=products[0][:, b - images[0], h, :],
+                        out=product[0][:, b - images[0], h, :],
                         lhsT=codes[:, h * P : (h + 1) * P].bitcast(FP8X4),
                         lhsT_scale=scales[:, h * P : (h + 1) * P],
                         rhs=w_codes[:].bitcast(FP8X4),
@@ -597,140 +503,101 @@ def tile_tokenmudule_pa_s_kernel(tc, patch_tokens, fc1_w, fc1_b, out):
             def add_bias():
                 nc.vector.tensor_tensor(
                     out=pre_act[:, images[0] : images[-1] + 1],
-                    in0=products[0][:],
+                    in0=product[0][:],
                     in1=bias[:].unsqueeze(1).unsqueeze(1).to_broadcast([P, len(images), H, F]),
                     op=ALU.add,
                 )
 
-            if not images:
-                return []
-            return [lambda b=b: quantise(b) for b in images] + [add_bias]
+            return [lambda b=b: quantise(b) for b in images] + [add_bias] if images else []
 
-        def gpsimd_products(b, pair):
-            for k in range(on_vector_count(b), OWN):
-                multiply(b, pair, k)
+        stored = out.rearrange("b (h p) f -> p b h f", p=P)
 
-        def round_ending(b):
-            for images in ROUNDS:
-                if images[-1] == b:
-                    return images
-            return ()
+        def finish(images):
+            these = slice(images[0], images[-1] + 1)
+            nc.scalar.activation(out=result[:, these], in_=pre_act[:, these], func=ACT.Gelu)
+            nc.sync.dma_start(out=stored[:, these], in_=result[:, these])
 
-        def norms(b, half, offsets=range(OWN)):
-            for k in offsets:
-                sum_products(b, k, half)
-
-        def preload(func):
-            nc.scalar.activation(out=unused[:], in_=one[:], func=func)
-
-        def run(main, between):
-            for step in main:
+        def run(steps):
+            for step in steps:
                 step()
-                for small in between[0:1]:
-                    small()
-                between = between[1:]
-            for small in between:
-                small()
 
-        def product_steps(b, pair):
-            return [lambda k=k: multiply(b, pair, k) for k in range(on_vector_count(b))]
+        def run_between(main, small):
+            for i, step in enumerate(main):
+                step()
+                run(small[i - SMALL_FROM : i - SMALL_FROM + 1] if i >= SMALL_FROM else [])
+            run(small[max(0, len(main) - SMALL_FROM) :])
 
-        def vector_phase(b, small, tasks, quantised):
-            first, second = product_steps(b, 0), product_steps(b, 1)
-            closing_steps = project_steps(quantised)
-            main = first + second[0:1]
-            main.append(lambda: clamp_on_vector(b, 0))
-            main += second[1:] + tasks[0:1]
-            main.append(lambda: clamp_on_vector(b, 1))
-            main += tasks[1:]
-            for i, step in enumerate(closing_steps):
+        def window(b, small, long, closing):
+            on_vector = V_CLAMPS_EVEN if b % 2 == 0 and b < B - 2 else ON_V
+
+            def products(pair):
+                return [
+                    lambda k=k: run([lambda ch=ch: multiply(b, ch, k) for ch in chunks_of(pair)])
+                    for k in range(ON_V)
+                ]
+
+            def clamps(pair):
+                return [lambda: clamp_on_vector(b, pair, on_vector)]
+
+            first, second = products(0), products(1)
+            main = first + second[0:1] + clamps(0) + second[1:] + long[0:1] + clamps(1) + long[1:]
+            for i, step in enumerate(closing):
                 main.insert(CLOSE_FROM + i if i < ROUND else BIAS_FROM, step)
-            run(main, [lambda: None] * SMALL_FROM + small)
-            for pair in range(CH // PAIR):
-                multiply(b, pair, OWN)
-                for k in list(range(on_vector_count(b), K)) + list(
-                    range(vector_clamps(b), on_vector_count(b))
-                ):
-                    clamp(b, pair, k)
-                window_sum(b, pair)
+            run_between(main, small)
 
-        def head_products(b, k):
-            di, dj = OFFSETS[k]
-            top = -di
-            lo, hi = max(0, -dj), GRID - max(0, dj)
-            rows, cols = GRID - top, hi - lo
-            grids = q[b][:].rearrange("p c (i j) -> p c i j", j=GRID)
-            products = head_pool.tile([P, CH, T], F32, name="head")
-            for pair in range(CH // PAIR):
-                chunks = slice(pair * PAIR, (pair + 1) * PAIR)
-                nc.gpsimd.tensor_tensor(
-                    out=products[:, chunks, 0 : rows * cols].rearrange(
-                        "p c (i j) -> p c i j", j=cols
-                    ),
-                    in0=grids[:, chunks, top:GRID, lo:hi],
-                    in1=grids[:, chunks, 0:rows, lo + dj : hi + dj],
-                    op=ALU.mult,
-                )
-                for ch in range(pair * PAIR, (pair + 1) * PAIR):
-                    unread = unread_pool.tile([P, T], BF16, name="unread_s")
-                    nc.scalar.activation(
-                        out=unread[:, 0 : rows * cols],
-                        in_=products[:, ch, 0 : rows * cols],
-                        func=ACT.Copy,
-                        accum_out=norm_sq_head[:, k - HEAD_FROM, ch : ch + 1],
-                    )
+            for pair in range(PAIRS):
+                square_own(b, pair)
+                for k in range(ON_V, K):
+                    for ch in chunks_of(pair):
+                        clamp(b, ch, k)
+                for k in range(on_vector, ON_V):
+                    relu(terms_of(b, pair)[:, k, :, -OFFSETS[k][0] * GRID : T])
+                for ch in chunks_of(pair):
+                    window_sum(b, ch)
 
         preload(ACT.Sqrt)
-        square_by_chunks(0)
-        transpose_q(0, 0)
-        copy_q(0, 0)
-        transpose_q(0, 1)
-        copy_q(0, 1)
+        square_first(0)
+        for pair in range(PAIRS):
+            transpose_q(0, pair)
+            copy_q(0, pair)
         square_x(1)
         transpose_x(0)
-        sum_squares(0, 0)
-        sum_squares(0, 1)
+        for pair in range(PAIRS):
+            sum_squares(0, pair)
         square_x(2)
-        for k in range(HEAD_FROM, OWN):
-            head_products(0, k)
-            if k == HEAD_FROM:
-                norms(0, 0, range(HEAD_FROM))
-                transpose_q(1, 0)
-                copy_q(1, 0)
+        sum_without_vector(0, HEAD_FROM)
+        sum_products(0, 0, range(HEAD_FROM))
+        transpose_q(1, 0)
+        copy_q(1, 0)
+        for k in range(HEAD_FROM + 1, OWN):
+            sum_without_vector(0, k)
         square_x(3)
         nc.gpsimd.memset(p_pad[:, 1], 0.0)
-        norms(0, 1, range(HEAD_FROM))
+        sum_products(0, 1, range(HEAD_FROM))
         transpose_q(1, 1)
-        nc.vector.tensor_copy(out=w_grouped[:], in_=w_raw[:].rearrange("p t f -> p f t"))
-        nc.vector.quantize_mx(
-            out=w_codes[:].bitcast(FP8X4),
-            scales=w_scales[:],
-            in_=w_grouped[:].rearrange("p f t -> p (f t)"),
-        )
-        start_coefficients(0)
+        quantise_weights()
+        take_roots(0)
 
         for b in range(-1, B - 2):
             small = coefficient_steps(b + 1)
-            tasks = add_x_tasks(round_ending(b - 1)) + scale_tokens_tasks(round_ending(b - 2))
+            long = add_x_steps(round_ending(b - 1)) + token_steps(round_ending(b - 2))
             copy_q(b + 2, 1)
             if b >= 0:
                 transpose_x(b + 1)
-                vector_phase(b, small, tasks, round_ending(b - 3))
-            for half in range(2):
-                sum_squares(b + 2, half)
+                window(b, small, long, linear_steps(round_ending(b - 3)))
+            for pair in range(PAIRS):
+                sum_squares(b + 2, pair)
             if b < 0:
                 for image in range(4, B):
                     square_x(image)
-                run([], small)
-            if b + 1 < B:
-                for pair in range(CH // PAIR):
-                    scale_cubes(b + 1, pair)
-                    gpsimd_products(b + 1, pair)
-            if b + 2 < B:
-                norms(b + 2, 0)
-                if b + 3 < B:
-                    transpose_q(b + 3, 0)
-            square_sums(round_ending(b - 1))
+                run(small)
+            for pair in range(PAIRS):
+                scale_cubes(b + 1, pair)
+                multiply_on_gpsimd(b + 1, pair)
+            sum_products(b + 2, 0)
+            if b + 3 < B:
+                transpose_q(b + 3, 0)
+            sum_round(round_ending(b - 1))
             summed = round_ending(b) if b < B - 3 else ()
             if summed:
                 preload(ACT.Ln)
@@ -739,72 +606,67 @@ def tile_tokenmudule_pa_s_kernel(tc, patch_tokens, fc1_w, fc1_b, out):
                 copy_q(b + 3, 0)
             exp_sum(summed)
             turn_tokens(round_ending(b - 2))
-            if b + 2 < B:
-                norms(b + 2, 1)
-                if b + 3 < B:
-                    transpose_q(b + 3, 1)
-            if b + 2 < B:
-                start_coefficients(b + 2)
-            roots(round_ending(b - 1))
-        def vector_products(b, pair, ks):
-            for k in ks:
-                multiply(b, pair, k)
+            sum_products(b + 2, 1)
+            if b + 3 < B:
+                transpose_q(b + 3, 1)
+            take_roots(b + 2)
+            take_r_roots(round_ending(b - 1))
 
         b = B - 2
-        transpose_x(b + 1)
-        vector_phase(b, coefficient_steps(b + 1), [], round_ending(b - 3))
-        pooled_of(round_ending(b - 1))
-        b = B - 1
-        for pair in range(CH // PAIR):
-            scale_cubes(b, pair)
-        for pair in range(CH // PAIR):
-            multiply(b, pair, OWN)
-            clamp(b, pair, OWN)
-        tasks = add_x_tasks(round_ending(b - 2))
-        previous = ()
+        early, last = round_ending(B - 3), B - 1
+
+        def clamp_last(ch):
+            clamp_on_vector(last, ch // PAIR, OWN, ch % PAIR)
+
+        transpose_x(last)
+        window(b, coefficient_steps(last), [], linear_steps(round_ending(b - 3)))
+        log_sum(early)
+        exp_sum(early)
+        for pair in range(PAIRS):
+            scale_cubes(last, pair)
+        for pair in range(PAIRS):
+            square_own(last, pair)
+            for ch in chunks_of(pair):
+                clamp(last, ch, OWN)
         for ch in range(CH):
-            for k in range(OWN):
-                multiply_chunk(b, ch, k)
-                if k == 0:
-                    for c in previous:
-                        clamp_chunk(b, c)
-                        window_chunk(b, c)
-            previous = (ch,)
-            if ch == 2:
-                for task in tasks:
-                    task()
-        square_sums(round_ending(b - 2))
-        roots(round_ending(b - 2))
-        for c in previous:
-            clamp_chunk(b, c)
-            window_chunk(b, c)
-        for task in scale_tokens_tasks(round_ending(b - 2)):
-            task()
-        log_sum((b - 1, b))
-        turn_tokens(round_ending(b - 2), on_vector=True)
-        steps = project_steps(round_ending(b - 2))
-        for step in steps[0:-1]:
-            step()
-        exp_sum((b, b - 1))
-        steps[-1]()
+            multiply(last, ch, 0)
+            if ch > 0:
+                clamp_last(ch - 1)
+                window_sum(last, ch - 1)
+            for k in range(1, OWN):
+                multiply(last, ch, k)
+            if ch == CH - 2:
+                run(add_x_steps(early))
+        sum_round(early)
+        take_r_roots(early)
+        clamp_last(CH - 1)
+        window_sum(last, CH - 1)
+        run(token_steps(early))
+        log_sum((b, last))
+        turn_tokens(early, on_vector=True)
+        steps = linear_steps(early)
+        run(steps[0:-1])
+        exp_sum((last, b))
+        run(steps[-1:])
         preload(ACT.Sqrt)
-        for image in (b, b - 1):
-            for task in add_x_tasks((image,)):
-                task()
-            square_sums_split(image)
-        roots((b, b - 1))
+        for image in (last, b):
+            run(add_x_steps((image,)))
+            start_r_sums(image)
+            sum_r_squares(image, 0, on_vector=True)
+            sum_r_squares(image, 1)
+        for image in (last, b):
+            take_r_roots((image,))
         preload(ACT.Gelu)
-        for image in (b, b - 1):
-            for task in scale_tokens_tasks((image,)):
-                task()
-        turn_tokens((b,), on_vector=True)
-        for first in range(0, B - 2, 2):
+        for image in (last, b):
+            run(token_steps((image,)))
+        turn_tokens((last,), on_vector=True)
+        for first in range(0, b, 2):
             finish((first, first + 1))
-        turn_tokens((b - 1,))
-        last, other = project_steps((b,)), project_steps((b - 1,))
-        last[0]()
-        other[0]()
-        last[1]()
+        turn_tokens((b,))
+        last_steps, other_steps = linear_steps((last,)), linear_steps((b,))
+        last_steps[0]()
+        other_steps[0]()
+        last_steps[1]()
+        finish((last,))
+        other_steps[1]()
         finish((b,))
-        other[1]()
-        finish((b - 1,))

from contextlib import ExitStack

import concourse.mybir as mybir
from concourse.masks import make_identity

F32 = mybir.dt.float32
BF16 = mybir.dt.bfloat16
U32 = mybir.dt.uint32
U8 = mybir.dt.uint8
FP8X4 = mybir.dt.float8_e4m3fn_x4
ALU = mybir.AluOpType
ACT = mybir.ActivationFunctionType

P = 128
B = 8
GRID = 16
T = GRID * GRID
H = T // P
C = 512
CH = C // P
PAIR = 2
PAIRS = CH // PAIR
F = 128
PACK = 4

FLOPS = 2 * B * T * C * F

OFFSETS = [(0, -1), (-1, 0), (-1, -1), (-1, 1), (-2, -1), (-2, 0), (-2, 1), (0, 0)]
K = len(OFFSETS)
OWN = OFFSETS.index((0, 0))
K_LEFT = OFFSETS.index((0, -1))
TERMS = [(k, 0) for k in range(K)] + [(K_LEFT, 1)]
MAX_TOP = 2

ON_V = 3
V_CLAMPS_EVEN = 1
HEAD_FROM = 5

SMALL_FROM = 6
CLOSE_FROM = 3
BIAS_FROM = 9

LEAD = 4
ROW = LEAD + GRID
PADDED = GRID * ROW + 8
TERM_COLS = T + 8
TERM_TILES = 5

EPS_GEM_CUBED = 1e-18
EPS_NORM_SQUARED = 1e-24
RATIO_SQUARED_MAX = 1e22

ROUNDS = [(0, 1), (2, 3), (4, 5), (6,), (7,)]
ROUND = 2


def tile_tokenmudule_pa_s_kernel(tc, patch_tokens, fc1_w, fc1_b, out):
    nc = tc.nc

    with ExitStack() as ctx:
        ctx.enter_context(tc.manual_schedule())

        def sbuf(name, bufs):
            return ctx.enter_context(tc.tile_pool(name=name, bufs=bufs))

        def psum(name, bufs):
            return ctx.enter_context(tc.psum_pool(name=name, bufs=bufs))

        keep = sbuf("keep", 1)
        nat_pool = sbuf("nat", B)
        head_pool = sbuf("head", 2)
        q_pool = sbuf("q", 3)
        unread_pool = sbuf("unread", 4)
        coef_pool = sbuf("coef", 3)
        pooled_pool = sbuf("pooled", 2 * ROUND)
        tail_pool = sbuf("tail", 2 * ROUND)
        xT_psum = psum("xT_psum", 1)
        qT_psum = psum("qT_psum", PAIRS)
        acc_psum = psum("acc_psum", ROUND * H)
        proj_psum = psum("proj_psum", 1)

        x_nat = keep.tile([P, B, H, C], BF16)
        for b in range(B):
            halves_of_b = patch_tokens[b].rearrange("(h p) c -> p h c", p=P)
            if b == 0:
                nc.sync.dma_start(out=x_nat[:, b, 0], in_=halves_of_b[:, 0])
                nc.scalar.dma_start(out=x_nat[:, b, 1], in_=halves_of_b[:, 1])
            else:
                nc.sync.dma_start(out=x_nat[:, b], in_=halves_of_b)
        w_raw = keep.tile([P, PACK, F], BF16)
        nc.scalar.dma_start(out=w_raw[:], in_=fc1_w.rearrange("(p t) f -> p t f", t=PACK))
        bias = keep.tile([P, F], BF16)
        nc.scalar.dma_start(out=bias[:], in_=fc1_b.partition_broadcast(P))

        ident_bf = keep.tile([P, P], BF16)
        make_identity(nc, ident_bf[:])
        ident_f = keep.tile([P, P], F32)
        make_identity(nc, ident_f[:])
        plus_eps = keep.tile([P, 1], F32)
        nc.vector.memset(plus_eps[:], EPS_GEM_CUBED)
        minus_eps = keep.tile([P, 1], F32)
        nc.vector.memset(minus_eps[:], -EPS_GEM_CUBED)
        one = keep.tile([P, 1], F32)
        nc.vector.memset(one[:], 1.0)
        unused = keep.tile([P, 1], F32)

        p_pad = keep.tile([P, 2, CH, PADDED], F32)
        nc.vector.memset(p_pad[:, 0], 0.0)
        term_tiles = [
            keep.tile([P, K, PAIR, TERM_COLS], F32, name="terms%d" % i) for i in range(TERM_TILES)
        ]
        for terms in term_tiles:
            nc.gpsimd.memset(terms[:, K_LEFT, :, T:TERM_COLS], 0.0)
            nc.gpsimd.memset(terms[:, 0:OWN, :, 0 : MAX_TOP * GRID], 0.0)

        w_grouped = keep.tile([P, F, PACK], BF16, align_bytes=64)
        w_codes = keep.tile([P, F], U32, align_bytes=64)
        w_scales = keep.tile([P, F], U8, align_bytes=64)
        norm_sq_head = keep.tile([P, OWN - HEAD_FROM, CH], F32)
        own_sq = keep.tile([P, B, CH], F32)
        pre_act = keep.tile([P, B, H, F], F32)
        result = keep.tile([P, B, H, F], F32)

        q_nat = {}
        xT = {}
        qT = {}
        q = {}
        norm_sq = {}
        norm = {}
        inv_norm = {}
        coef = {}
        acc = {}
        pooled = {}
        r_sq, r_norm = {}, {}
        tokens = {}
        grouped = {}

        def preload(func):
            nc.scalar.activation(out=unused[:], in_=one[:], func=func)

        def round_ending(b):
            for images in ROUNDS:
                if images[-1] == b:
                    return images
            return ()

        def grid(ap):
            return ap.rearrange("p (i j) -> p i j", j=GRID)

        def grids(ap):
            return ap.rearrange("p c (i j) -> p c i j", j=GRID)

        def chunks_of(pair):
            return range(pair * PAIR, (pair + 1) * PAIR)

        def square_x(b):
            q_nat[b] = nat_pool.tile([P, H, C], F32, name="q_nat")
            nc.scalar.activation(out=q_nat[b][:], in_=x_nat[:, b], func=ACT.Square)

        def square_first(b):
            q_nat[b] = nat_pool.tile([P, H, C], F32, name="q_nat")
            for ch in range(CH):
                square = q_nat[b][:, :, ch * P : (ch + 1) * P]
                x = x_nat[:, b, :, ch * P : (ch + 1) * P]
                if ch % 2 == 0:
                    nc.scalar.activation(out=square, in_=x, func=ACT.Square)
                else:
                    nc.vector.tensor_tensor(out=square, in0=x, in1=x, op=ALU.mult)

        def transpose_x(b):
            xT[b] = xT_psum.tile([P, CH, T], BF16, name="xT")
            for h in range(H):
                for ch in range(CH):
                    nc.tensor.transpose(
                        xT[b][:, ch, h * P : (h + 1) * P],
                        x_nat[:, b, h, ch * P : (ch + 1) * P],
                        ident_bf[:],
                    )

        def transpose_q(b, pair):
            qT[b, pair] = qT_psum.tile([P, PAIR, T], F32, name="qT")
            for ch in chunks_of(pair):
                for h in range(H):
                    nc.tensor.transpose(
                        qT[b, pair][:, ch % PAIR, h * P : (h + 1) * P],
                        q_nat[b][:, h, ch * P : (ch + 1) * P],
                        ident_f[:],
                    )

        def copy_q(b, pair):
            if pair == 0:
                q[b] = q_pool.tile([P, CH, T], F32, name="q")
            nc.scalar.copy(out=q[b][:, pair * PAIR : (pair + 1) * PAIR, :], in_=qT[b, pair][:])

        def sum_squares(b, pair):
            for ch in chunks_of(pair):
                unread = unread_pool.tile([P, T], BF16, name="unread_s")
                nc.scalar.activation(
                    out=unread[:],
                    in_=q[b][:, ch],
                    func=ACT.Square,
                    accum_out=own_sq[:, b, ch : ch + 1],
                )

        def overlap(k):
            di, dj = OFFSETS[k]
            lo, hi = max(0, -dj), GRID - max(0, dj)
            here = (slice(-di, GRID), slice(lo, hi))
            there = (slice(0, GRID + di), slice(lo + dj, hi + dj))
            return here, there, GRID + di, hi - lo

        def sum_products(b, pair, offsets=range(OWN)):
            if b not in norm_sq:
                norm_sq[b] = coef_pool.tile([P, K, CH], F32, name="norm_sq")
            for k in offsets:
                here, there, rows, cols = overlap(k)
                for ch in chunks_of(pair):
                    unread = unread_pool.tile([P, T], F32, name="unread_v")
                    nc.vector.scalar_tensor_tensor(
                        out=unread[:, 0 : rows * cols].rearrange("p (i j) -> p i j", j=cols),
                        in0=grid(qT[b, pair][:, ch % PAIR, :])[:, here[0], here[1]],
                        scalar=1.0,
                        in1=grid(q[b][:, ch, :])[:, there[0], there[1]],
                        op0=ALU.mult,
                        op1=ALU.mult,
                        accum_out=norm_sq[b][:, k, ch : ch + 1],
                    )

        def sum_without_vector(b, k):
            here, there, rows, cols = overlap(k)
            products = head_pool.tile([P, CH, T], F32, name="head")
            for pair in range(PAIRS):
                these = slice(pair * PAIR, (pair + 1) * PAIR)
                nc.gpsimd.tensor_tensor(
                    out=products[:, these, 0 : rows * cols].rearrange(
                        "p c (i j) -> p c i j", j=cols
                    ),
                    in0=grids(q[b][:])[:, these, here[0], here[1]],
                    in1=grids(q[b][:])[:, these, there[0], there[1]],
                    op=ALU.mult,
                )
                for ch in chunks_of(pair):
                    unread = unread_pool.tile([P, T], BF16, name="unread_s")
                    nc.scalar.activation(
                        out=unread[:, 0 : rows * cols],
                        in_=products[:, ch, 0 : rows * cols],
                        func=ACT.Copy,
                        accum_out=norm_sq_head[:, k - HEAD_FROM, ch : ch + 1],
                    )

        def take_roots(b):
            floored = coef_pool.tile([P, K, CH], F32, name="n_floored")
            on_vector = HEAD_FROM if b == 0 else OWN
            sums = [
                (floored[:, OWN, :], own_sq[:, b, :]),
                (floored[:, 0:on_vector, :], norm_sq[b][:, 0:on_vector, :]),
            ]
            if b == 0:
                sums.append((floored[:, HEAD_FROM:OWN, :], norm_sq_head[:]))
            for to, total in sums:
                nc.vector.tensor_scalar_max(to, total, EPS_NORM_SQUARED)
            norm[b] = coef_pool.tile([P, K, CH], F32, name="norm")
            nc.scalar.activation(out=norm[b][:], in_=floored[:], func=ACT.Sqrt)

        def coefficient_steps(b):
            inv_norm[b] = coef_pool.tile([P, K, CH], F32, name="inv_norm")
            ratio = coef_pool.tile([P, K, CH], F32, name="ratio")
            ratio_sq = coef_pool.tile([P, K, CH], F32, name="ratio_sq")
            coef[b] = coef_pool.tile([P, K, CH], F32, name="coef")
            return [
                lambda: nc.vector.reciprocal(inv_norm[b][:], norm[b][:]),
                lambda: nc.vector.tensor_tensor(
                    out=ratio[:],
                    in0=inv_norm[b][:],
                    in1=norm[b][:, OWN : OWN + 1, :].to_broadcast([P, K, CH]),
                    op=ALU.mult,
                ),
                lambda: nc.vector.tensor_tensor(
                    out=ratio_sq[:], in0=ratio[:], in1=ratio[:], op=ALU.mult
                ),
                lambda: nc.vector.scalar_tensor_tensor(
                    out=coef[b][:],
                    in0=ratio_sq[:],
                    scalar=RATIO_SQUARED_MAX,
                    in1=inv_norm[b][:],
                    op0=ALU.min,
                    op1=ALU.mult,
                ),
            ]

        def padded_rows(b, chunks, dj):
            first = LEAD + dj
            flat = p_pad[:, b % 2, chunks, first : first + GRID * ROW]
            return flat.rearrange("p c (i j) -> p c i j", j=ROW)[:, :, :, 0:GRID]

        def scale_cubes(b, pair):
            for ch in chunks_of(pair):
                nc.vector.scalar_tensor_tensor(
                    out=padded_rows(b, slice(ch, ch + 1), 0)[:, 0],
                    in0=grid(q[b][:, ch, :]),
                    scalar=inv_norm[b][:, OWN, ch : ch + 1],
                    in1=grid(xT[b][:, ch, :]),
                    op0=ALU.mult,
                    op1=ALU.mult,
                )

        def terms_of(b, pair):
            return term_tiles[(b * PAIRS + pair) % TERM_TILES]

        def product_parts(b, pair, first, last, k):
            di, dj = OFFSETS[k]
            chunks = slice(pair * PAIR + first, pair * PAIR + last)
            return (
                grids(terms_of(b, pair)[:, k, first:last, -di * GRID : T]),
                padded_rows(b, chunks, 0)[:, :, -di:GRID, :],
                padded_rows(b, chunks, dj)[:, :, 0 : GRID + di, :],
            )

        def multiply(b, ch, k):
            c = ch % PAIR
            product, here, there = product_parts(b, ch // PAIR, c, c + 1, k)
            nc.vector.scalar_tensor_tensor(
                out=product[:, 0],
                in0=here[:, 0],
                scalar=coef[b][:, k, ch : ch + 1],
                in1=there[:, 0],
                op0=ALU.mult,
                op1=ALU.mult,
            )

        def multiply_on_gpsimd(b, pair):
            for k in range(ON_V, OWN):
                product, here, there = product_parts(b, pair, 0, PAIR, k)
                nc.gpsimd.tensor_tensor(out=product, in0=here, in1=there, op=ALU.mult)

        def square_own(b, pair):
            product, here, _ = product_parts(b, pair, 0, PAIR, OWN)
            nc.scalar.activation(out=product, in_=here, func=ACT.Square)

        def relu(terms, scale=1.0):
            nc.scalar.activation(
                out=terms, in_=terms, func=ACT.Relu, scale=scale, bias=minus_eps[:]
            )

        def clamp(b, ch, k):
            terms = terms_of(b, ch // PAIR)[:, k, ch % PAIR, -OFFSETS[k][0] * GRID : T]
            relu(terms, coef[b][:, k, ch : ch + 1])

        def clamp_on_vector(b, pair, last, chunks=slice(0, PAIR)):
            terms = terms_of(b, pair)[:, 0:last, chunks, 0:T]
            nc.vector.tensor_scalar(terms, terms, -EPS_GEM_CUBED, 0.0, op0=ALU.add, op1=ALU.max)

        def window_sum(b, ch):
            for h in range(H):
                if (b, h) not in acc:
                    if b == B - 2:
                        acc[b, h] = qT_psum.tile([P, C], F32, name="qT")
                    else:
                        acc[b, h] = acc_psum.tile([P, C], F32, name="acc")
            terms = terms_of(b, ch // PAIR)
            for i, (k, ahead) in enumerate(TERMS):
                for h in range(H):
                    nc.tensor.matmul(
                        acc[b, h][:, ch * P : (ch + 1) * P],
                        lhsT=terms[:, k, ch % PAIR, ahead + h * P : ahead + (h + 1) * P],
                        rhs=ident_f[:],
                        is_transpose=True,
                        start=(i == 0),
                        stop=(i == len(TERMS) - 1),
                    )

        def halves(b):
            return [slice(0, 1), slice(1, 2)] if b >= B - 2 else [slice(0, 2)]

        def log_sum(images):
            for b in images:
                pooled[b] = pooled_pool.tile([P, H, C], F32, name="pooled")
                for h in range(H):
                    nc.scalar.activation(
                        out=pooled[b][:, h, :],
                        in_=acc[b, h][:],
                        func=ACT.Ln,
                        scale=1.0 / len(TERMS),
                        bias=plus_eps[:],
                    )

        def exp_sum(images):
            for b in images:
                for h in halves(b):
                    nc.scalar.activation(
                        out=pooled[b][:, h], in_=pooled[b][:, h], func=ACT.Exp, scale=1.0 / 3.0
                    )

        def add_x_steps(images):
            return [
                lambda b=b, h=h: nc.vector.tensor_tensor(
                    out=pooled[b][:, h], in0=pooled[b][:, h], in1=x_nat[:, b, h], op=ALU.add
                )
                for b in images
                for h in halves(b)
            ]

        def start_r_sums(b):
            r_sq[b] = tail_pool.tile([P, H], F32, name="r_sq")

        def sum_r_squares(b, h, on_vector=False):
            unread = unread_pool.tile([P, C], BF16, name="unread_r")
            r, total = pooled[b][:, h, :], r_sq[b][:, h : h + 1]
            if on_vector:
                nc.vector.scalar_tensor_tensor(
                    out=unread[:], in0=r, scalar=1.0, in1=r, op0=ALU.mult, op1=ALU.mult, accum_out=total
                )
            else:
                nc.scalar.activation(out=unread[:], in_=r, func=ACT.Square, accum_out=total)

        def sum_round(images):
            for b in images:
                start_r_sums(b)
                for h in range(H):
                    sum_r_squares(b, h)

        def take_r_roots(images):
            for b in images:
                floored = tail_pool.tile([P, H], F32, name="r_floored")
                nc.vector.tensor_scalar_max(floored[:], r_sq[b][:], EPS_NORM_SQUARED)
                r_norm[b] = tail_pool.tile([P, H], F32, name="r_norm")
                nc.scalar.activation(out=r_norm[b][:], in_=floored[:], func=ACT.Sqrt)

        def token_steps(images):
            inverses, products = [], []
            for b in images:
                inv_r = tail_pool.tile([P, H], F32, name="inv_r")
                inverses.append(
                    lambda b=b, inv_r=inv_r: nc.vector.reciprocal(inv_r[:], r_norm[b][:])
                )
                tokens[b] = tail_pool.tile([P, H, C], BF16, name="tokens")
                for h in range(H):
                    products.append(
                        lambda b=b, h=h, inv_r=inv_r: nc.vector.tensor_scalar_mul(
                            tokens[b][:, h, :], pooled[b][:, h, :], inv_r[:, h : h + 1]
                        )
                    )
            return inverses + products

        def turn_tokens(images, on_vector=False):
            for b in images:
                words = tokens[b][:].rearrange("p h c -> p (h c)").bitcast(F32)
                if b in ROUNDS[0]:
                    tokT = acc_psum.tile([P, H, 2, P], F32, name="acc")
                elif b < B - 4 or b % 2 == 0:
                    tokT = proj_psum.tile([P, H, 2, P], F32, name="proj")
                else:
                    tokT = xT_psum.tile([P, H, 2, P], F32, name="xT")
                for h in range(H):
                    for u in range(2):
                        nc.tensor.transpose(
                            tokT[:, h, u, :],
                            words[:, h * (C // 2) + u : (h + 1) * (C // 2) : 2],
                            ident_f[:],
                        )
                grouped[b] = tail_pool.tile(
                    [P, H * P * PACK], BF16, name="grouped", align_bytes=64
                )
                copy = nc.vector.tensor_copy if on_vector else nc.scalar.copy
                copy(
                    out=grouped[b][:].bitcast(F32).rearrange("p (h r u) -> p h r u", h=H, u=2),
                    in_=tokT[:].rearrange("p h u r -> p h r u"),
                )

        def quantise_weights():
            nc.vector.tensor_copy(out=w_grouped[:], in_=w_raw[:].rearrange("p t f -> p f t"))
            nc.vector.quantize_mx(
                out=w_codes[:].bitcast(FP8X4),
                scales=w_scales[:],
                in_=w_grouped[:].rearrange("p f t -> p (f t)"),
            )

        def linear_steps(images):
            product = {}

            def quantise(b):
                if b == images[0]:
                    if b == B - 1:
                        product[0] = xT_psum.tile([P, 1, H, F], F32, name="xT")
                    else:
                        product[0] = proj_psum.tile([P, len(images), H, F], F32, name="proj")
                codes = tail_pool.tile([P, H * P], U32, name="codes", align_bytes=64)
                scales = tail_pool.tile([P, H * P], U8, name="scales", align_bytes=64)
                nc.vector.quantize_mx(
                    out=codes[:].bitcast(FP8X4), scales=scales[:], in_=grouped[b][:]
                )
                for h in range(H):
                    nc.tensor.matmul_mx(
                        out=product[0][:, b - images[0], h, :],
                        lhsT=codes[:, h * P : (h + 1) * P].bitcast(FP8X4),
                        lhsT_scale=scales[:, h * P : (h + 1) * P],
                        rhs=w_codes[:].bitcast(FP8X4),
                        rhs_scale=w_scales[:],
                        start=True,
                        stop=True,
                    )

            def add_bias():
                nc.vector.tensor_tensor(
                    out=pre_act[:, images[0] : images[-1] + 1],
                    in0=product[0][:],
                    in1=bias[:].unsqueeze(1).unsqueeze(1).to_broadcast([P, len(images), H, F]),
                    op=ALU.add,
                )

            return [lambda b=b: quantise(b) for b in images] + [add_bias] if images else []

        stored = out.rearrange("b (h p) f -> p b h f", p=P)

        def finish(images):
            these = slice(images[0], images[-1] + 1)
            nc.scalar.activation(out=result[:, these], in_=pre_act[:, these], func=ACT.Gelu)
            nc.sync.dma_start(out=stored[:, these], in_=result[:, these])

        def run(steps):
            for step in steps:
                step()

        def run_between(main, small):
            for i, step in enumerate(main):
                step()
                run(small[i - SMALL_FROM : i - SMALL_FROM + 1] if i >= SMALL_FROM else [])
            run(small[max(0, len(main) - SMALL_FROM) :])

        def window(b, small, long, closing):
            on_vector = V_CLAMPS_EVEN if b % 2 == 0 and b < B - 2 else ON_V

            def products(pair):
                return [
                    lambda k=k: run([lambda ch=ch: multiply(b, ch, k) for ch in chunks_of(pair)])
                    for k in range(ON_V)
                ]

            def clamps(pair):
                return [lambda: clamp_on_vector(b, pair, on_vector)]

            first, second = products(0), products(1)
            main = first + second[0:1] + clamps(0) + second[1:] + long[0:1] + clamps(1) + long[1:]
            for i, step in enumerate(closing):
                main.insert(CLOSE_FROM + i if i < ROUND else BIAS_FROM, step)
            run_between(main, small)

            for pair in range(PAIRS):
                square_own(b, pair)
                for k in range(ON_V, K):
                    for ch in chunks_of(pair):
                        clamp(b, ch, k)
                for k in range(on_vector, ON_V):
                    relu(terms_of(b, pair)[:, k, :, -OFFSETS[k][0] * GRID : T])
                for ch in chunks_of(pair):
                    window_sum(b, ch)

        preload(ACT.Sqrt)
        square_first(0)
        for pair in range(PAIRS):
            transpose_q(0, pair)
            copy_q(0, pair)
        square_x(1)
        transpose_x(0)
        for pair in range(PAIRS):
            sum_squares(0, pair)
        square_x(2)
        sum_without_vector(0, HEAD_FROM)
        sum_products(0, 0, range(HEAD_FROM))
        transpose_q(1, 0)
        copy_q(1, 0)
        for k in range(HEAD_FROM + 1, OWN):
            sum_without_vector(0, k)
        square_x(3)
        nc.gpsimd.memset(p_pad[:, 1], 0.0)
        sum_products(0, 1, range(HEAD_FROM))
        transpose_q(1, 1)
        quantise_weights()
        take_roots(0)

        for b in range(-1, B - 2):
            small = coefficient_steps(b + 1)
            long = add_x_steps(round_ending(b - 1)) + token_steps(round_ending(b - 2))
            copy_q(b + 2, 1)
            if b >= 0:
                transpose_x(b + 1)
                window(b, small, long, linear_steps(round_ending(b - 3)))
            for pair in range(PAIRS):
                sum_squares(b + 2, pair)
            if b < 0:
                for image in range(4, B):
                    square_x(image)
                run(small)
            for pair in range(PAIRS):
                scale_cubes(b + 1, pair)
                multiply_on_gpsimd(b + 1, pair)
            sum_products(b + 2, 0)
            if b + 3 < B:
                transpose_q(b + 3, 0)
            sum_round(round_ending(b - 1))
            summed = round_ending(b) if b < B - 3 else ()
            if summed:
                preload(ACT.Ln)
            log_sum(summed)
            if b + 3 < B:
                copy_q(b + 3, 0)
            exp_sum(summed)
            turn_tokens(round_ending(b - 2))
            sum_products(b + 2, 1)
            if b + 3 < B:
                transpose_q(b + 3, 1)
            take_roots(b + 2)
            take_r_roots(round_ending(b - 1))

        b = B - 2
        early, last = round_ending(B - 3), B - 1

        def clamp_last(ch):
            clamp_on_vector(last, ch // PAIR, OWN, ch % PAIR)

        transpose_x(last)
        window(b, coefficient_steps(last), [], linear_steps(round_ending(b - 3)))
        log_sum(early)
        exp_sum(early)
        for pair in range(PAIRS):
            scale_cubes(last, pair)
        for pair in range(PAIRS):
            square_own(last, pair)
            for ch in chunks_of(pair):
                clamp(last, ch, OWN)
        for ch in range(CH):
            multiply(last, ch, 0)
            if ch > 0:
                clamp_last(ch - 1)
                window_sum(last, ch - 1)
            for k in range(1, OWN):
                multiply(last, ch, k)
            if ch == CH - 2:
                run(add_x_steps(early))
        sum_round(early)
        take_r_roots(early)
        clamp_last(CH - 1)
        window_sum(last, CH - 1)
        run(token_steps(early))
        log_sum((b, last))
        turn_tokens(early, on_vector=True)
        steps = linear_steps(early)
        run(steps[0:-1])
        exp_sum((last, b))
        run(steps[-1:])
        preload(ACT.Sqrt)
        for image in (last, b):
            run(add_x_steps((image,)))
            start_r_sums(image)
            sum_r_squares(image, 0, on_vector=True)
            sum_r_squares(image, 1)
        for image in (last, b):
            take_r_roots((image,))
        preload(ACT.Gelu)
        for image in (last, b):
            run(token_steps((image,)))
        turn_tokens((last,), on_vector=True)
        for first in range(0, b, 2):
            finish((first, first + 1))
        turn_tokens((b,))
        last_steps, other_steps = linear_steps((last,)), linear_steps((b,))
        last_steps[0]()
        other_steps[0]()
        last_steps[1]()
        finish((last,))
        other_steps[1]()
        finish((b,))
